import numpy as np
import ml_dtypes


def mxq(x, axis, fmt="e4m3"):
    dtype, down = {"e4m3": (ml_dtypes.float8_e4m3fn, 7), "e5m2": (ml_dtypes.float8_e5m2, 14)}[fmt]
    v = np.moveaxis(np.asarray(x, np.float32).astype(ml_dtypes.bfloat16).astype(np.float64), axis, -1)
    blocks = v.reshape(v.shape[:-1] + (-1, 32))
    amax = np.abs(blocks).max(-1, keepdims=True)
    byte = np.maximum(np.where(amax > 0, np.frexp(amax)[1] - 1 + 127, 0) - down, 1)
    scale = np.exp2(byte - 127.0)
    codes = (blocks / scale).astype(np.float32).astype(dtype).astype(np.float64)
    return np.moveaxis((codes * scale).reshape(v.shape), -1, axis)


WIDE = False


def mx_kscale(k):
    if not WIDE:
        return np.ones(k)
    levels = np.array([10, -10, 5, -5, 0])
    if k % 512:
        return np.exp2(np.random.permutation(np.resize(levels, k // 32))).repeat(32)
    a = np.empty((k // 512, 16))
    for p in range(k // 512):
        a[p, :8] = np.random.permutation(np.resize(levels, 8))
        for g in range(8):
            far = levels[np.abs(levels - a[p, g]) >= 10]
            a[p, g + 8] = far[np.random.randint(len(far))]
    return np.exp2(a.ravel()).repeat(32)


BF16 = ml_dtypes.bfloat16


def bf(x):
    return np.asarray(x, np.float32).astype(BF16)


def f64(x):
    return np.asarray(x).astype(np.float64)


B, T, D, DV = 1, 2048, 128, 256


def sigmoid(u):
    return 1.0 / (1.0 + np.exp(-u))


def setup_inputs():
    s = mx_kscale(T)
    q = np.random.standard_normal((B, T, D)) * 1.6
    k = np.random.standard_normal((B, T, D)) * 1.6
    q[..., 0] = 4.0
    q[..., 1] = -4.0
    k[..., 0] += np.log(s)[None, :] * np.sqrt(D) / 4.0
    v = np.random.standard_normal((B, T, DV)) * s[None, :, None] * np.mean(1.0 / s)
    return {"q": bf(q),
            "k": bf(k),
            "v": bf(v),
            "mask": (np.random.random((1, T, T)) < 0.7).astype(np.int32),
            "mode": bf(0.5 + 0.3 * np.random.standard_normal(1))}


def reference(q, k, v, mask, mode):
    q, k, v = f64(q), f64(k), f64(v)
    scale = D ** (-0.5)
    meson = -(q @ k.transpose(0, 2, 1)) * scale
    k_perm = np.roll(k, 1, axis=-1)
    baryon = (q @ k_perm.transpose(0, 2, 1)) * scale
    alpha = sigmoid(f64(mode))
    attn = alpha * meson + (1.0 - alpha) * baryon
    attn = np.where(f64(mask) == 0.0, -np.inf, attn)
    e = np.exp(attn - attn.max(-1, keepdims=True))
    return (mxq(e, 2, "e4m3") @ mxq(v, 1, "e4m3")) / e.sum(-1, keepdims=True)

@@ -1,0 +1,272 @@
+import math
+
+import concourse.mybir as mybir
+from concourse.masks import make_identity
+
+F32 = mybir.dt.float32
+BF16 = mybir.dt.bfloat16
+I32 = mybir.dt.int32
+U32 = mybir.dt.uint32
+U8 = mybir.dt.uint8
+FP8X4 = mybir.dt.float8_e4m3fn_x4
+ALU = mybir.AluOpType
+ACT = mybir.ActivationFunctionType
+
+P = 128
+T = 2048
+D = 128
+DV = 256
+PACK = 4
+K_PASS = P * PACK
+N_PASS = T // K_PASS
+N_TILES = T // P
+BANK = 512
+N_BANKS = T // BANK
+GROUP = 2
+N_GROUPS = N_TILES // GROUP
+MASKS_AHEAD = 3
+
+SHRINK = 2.0 ** -40
+GROW = 2.0 ** 40
+
+FLOPS = 2 * (2 * T * T * D) + 2 * T * T * DV
+
+
+def tile_dualmodehead_kernel(tc, q, k, v, mask, mode, out):
+    nc = tc.nc
+    q_rows = q.flatten_outer_dims().rearrange("(p n) d -> p n d", n=N_TILES)
+    k_rows = k.flatten_outer_dims().rearrange("(j p) d -> p j d", p=P)
+    v_rows = v.flatten_outer_dims().rearrange("(c p t) w -> p c t w", p=P, t=PACK)
+    mask_tiles = mask.bitcast(I32).flatten_outer_dims().rearrange("(p n) (k w) -> n p k w", n=N_TILES, w=2)
+    out_tiles = out.flatten_outer_dims().rearrange("(p n) w -> n p w", n=N_TILES)
+
+    with tc.tile_pool(name="keep", bufs=1) as keep, \
+            tc.tile_pool(name="prep", bufs=N_GROUPS) as prep, \
+            tc.tile_pool(name="mask_pool", bufs=MASKS_AHEAD + 1) as mask_pool, \
+            tc.tile_pool(name="work", bufs=3) as work, \
+            tc.tile_pool(name="small", bufs=6) as small, \
+            tc.psum_pool(name="score_psum", bufs=N_BANKS) as score_psum, \
+            tc.psum_pool(name="turn_psum", bufs=3) as turn_psum, \
+            tc.psum_pool(name="out_psum", bufs=1) as out_psum, \
+            tc.manual_schedule():
+
+        mask_of, score_of, shifted_of, row_max_of, row_sum_of = {}, {}, {}, {}, {}
+        e_of, turned_of, grouped_of, codes_of, scales_of, acc_of, inv_sum_of = {}, {}, {}, {}, {}, {}, {}
+
+        def load_mask(n):
+            if not 0 <= n < N_TILES:
+                return
+            mask_of[n] = mask_pool.tile([P, T, 2], I32, name="mask_sb")
+            for h in range(2):
+                keys = slice(T // 2 * h, T // 2 * (h + 1))
+                nc.sync.dma_start(out=mask_of[n][:, keys, :], in_=mask_tiles[n][:, keys, :])
+
+        mode_sb = keep.tile([P, 1], BF16)
+        nc.sync.dma_start(out=mode_sb[:], in_=mode.partition_broadcast(P))
+        q_ext = keep.tile([P, N_TILES, D + 1], BF16)
+        nc.sync.dma_start(out=q_ext[:, :, 0:D], in_=q_rows)
+        k_sb = keep.tile([P, N_TILES, D], BF16)
+        nc.sync.dma_start(out=k_sb[:], in_=k_rows)
+        load_mask(0)
+        v_raw = keep.tile([P, N_PASS, PACK, DV], BF16)
+        nc.sync.dma_start(out=v_raw[:], in_=v_rows)
+        load_mask(1)
+
+        ident = keep.tile([P, P], BF16)
+        make_identity(nc, ident[:])
+        minus_one = keep.tile([P, 1], F32)
+        nc.gpsimd.memset(minus_one[:], -1.0)
+
+        exp_neg = keep.tile([P, 1], F32)
+        nc.scalar.activation(out=exp_neg[:], in_=mode_sb[:], func=ACT.Exp, scale=-1.0)
+        denom = keep.tile([P, 1], F32)
+        nc.vector.tensor_scalar_add(out=denom[:], in0=exp_neg[:], scalar1=1.0)
+        alpha = keep.tile([P, 1], F32)
+        nc.vector.reciprocal(out=alpha[:], in_=denom[:])
+        unit = SHRINK / math.sqrt(D)
+        w_meson = keep.tile([P, 1], F32)
+        nc.vector.tensor_scalar_mul(out=w_meson[:], in0=alpha[:], scalar1=unit)
+        w_baryon = keep.tile([P, 1], F32)
+        nc.vector.tensor_scalar(out=w_baryon[:], in0=alpha[:], scalar1=-unit, scalar2=unit,
+                                op0=ALU.mult, op1=ALU.add)
+
+        nc.scalar.copy(out=q_ext[:, :, D:D + 1], in_=q_ext[:, :, 0:1])
+        qT = keep.tile([P, N_TILES, 2, P], BF16)
+        kT = keep.tile([P, T], BF16)
+
+        blend_of, high_of, low_of = {}, {}, {}
+
+        def blend_queries(g):
+            tiles = slice(GROUP * g, GROUP * (g + 1))
+            blend_of[g] = prep.tile([P, GROUP, D], F32, name="blend")
+            nc.vector.scalar_tensor_tensor(out=blend_of[g][:], in0=q_ext[:, tiles, 1:D + 1],
+                                           scalar=w_baryon[:, 0:1], in1=meson_of[g][:],
+                                           op0=ALU.mult, op1=ALU.subtract)
+            high_of[g] = prep.tile([P, GROUP, D], BF16, name="high")
+            nc.vector.scalar_tensor_tensor(out=high_of[g][:], in0=q_ext[:, tiles, 1:D + 1],
+                                           scalar=w_baryon[:, 0:1], in1=meson_of[g][:],
+                                           op0=ALU.mult, op1=ALU.subtract)
+            low_of[g] = prep.tile([P, GROUP, D], BF16, name="low")
+            nc.gpsimd.tensor_tensor(out=low_of[g][:], in0=blend_of[g][:], in1=high_of[g][:], op=ALU.subtract)
+
+        def turn_queries(g):
+            tiles = slice(GROUP * g, GROUP * (g + 1))
+            turned = turn_psum.tile([P, GROUP, 2, P], BF16, tag="turned")
+            for i in range(GROUP):
+                nc.tensor.transpose(turned[:, i, 0, :], high_of[g][:, i, :], ident[:])
+            for i in range(GROUP):
+                nc.tensor.transpose(turned[:, i, 1, :], low_of[g][:, i, :], ident[:])
+            nc.scalar.copy(out=qT[:, tiles, :, :], in_=turned[:])
+
+        def turn_keys(h):
+            turned = turn_psum.tile([P, 8, P], BF16, tag="turned")
+            for j in range(8):
+                nc.tensor.transpose(turned[:, j, :], k_sb[:, 8 * h + j, :], ident[:])
+            nc.scalar.copy(out=kT[:, 1024 * h:1024 * (h + 1)], in_=turned[:].rearrange("p j c -> p (j c)"))
+
+        meson_of = {}
+        for g in range(N_GROUPS):
+            meson_of[g] = prep.tile([P, GROUP, D], F32, name="meson_part")
+            nc.scalar.activation(out=meson_of[g][:], in_=q_ext[:, GROUP * g:GROUP * (g + 1), 0:D], func=ACT.Copy,
+                                 scale=w_meson[:, 0:1])
+        for g in range(N_GROUPS):
+            blend_queries(g)
+
+        v_grouped = keep.tile([P, N_PASS, DV, PACK], BF16, align_bytes=64)
+        v_codes = keep.tile([P, N_PASS, DV], U32, align_bytes=64)
+        v_scales = keep.tile([P, N_PASS, DV], U8, align_bytes=64)
+        for c in range(N_PASS):
+            nc.gpsimd.tensor_scalar(out=v_grouped[:, c], in0=v_raw[:, c].rearrange("p t w -> p w t"),
+                                    scalar1=1.0, scalar2=0.0, op0=ALU.mult, op1=ALU.add)
+
+        def quantise_v():
+            nc.vector.quantize_mx(out=v_codes[:].rearrange("p c w -> p (c w)").bitcast(FP8X4),
+                                  scales=v_scales[:].rearrange("p c w -> p (c w)"),
+                                  in_=v_grouped[:].rearrange("p c w t -> p (c w t)"))
+
+        def scores(n, b):
+            if not 0 <= n < N_TILES:
+                return
+            cols = slice(BANK * b, BANK * (b + 1))
+            score_of[n, b] = score_psum.tile([P, BANK], F32, name="score")
+            nc.tensor.matmul(score_of[n, b][:], lhsT=qT[:, n, 0, :], rhs=kT[:, cols], start=True, stop=False)
+            nc.tensor.matmul(score_of[n, b][:], lhsT=qT[:, n, 1, :], rhs=kT[:, cols], start=False, stop=True)
+
+        def mask_scores(n, b):
+            if not 0 <= n < N_TILES:
+                return
+            cols = slice(BANK * b, BANK * (b + 1))
+            if b == 0:
+                shifted_of[n] = work.tile([P, T], F32, name="shifted")
+            nc.vector.scalar_tensor_tensor(out=shifted_of[n][:, cols], in0=mask_of[n][:, cols, 0], scalar=1.0,
+                                           in1=score_of[n, b][:], op0=ALU.subtract, op1=ALU.add)
+
+        def row_max(n):
+            if not 0 <= n < N_TILES:
+                return
+            row_max_of[n] = small.tile([P, 1], F32, name="row_max")
+            nc.vector.tensor_reduce(out=row_max_of[n][:], in_=shifted_of[n][:], axis=mybir.AxisListType.X, op=ALU.max)
+
+        def exponent(n):
+            if not 0 <= n < N_TILES:
+                return
+            neg_max = small.tile([P, 1], F32)
+            nc.scalar.mul(out=neg_max[:], in_=row_max_of[n][:], mul=-GROW)
+            e_of[n] = work.tile([P, T], BF16, name="e_sb")
+            row_sum_of[n] = small.tile([P, 1], F32, name="row_sum")
+            nc.scalar.activation(out=e_of[n][:].rearrange("p (t i) -> p t i", t=PACK),
+                                 in_=shifted_of[n][:].rearrange("p (i t) -> p t i", t=PACK), func=ACT.Exp, bias=neg_max[:, 0:1],
+                                 scale=GROW, accum_out=row_sum_of[n][:])
+            inv_sum_of[n] = small.tile([P, 1], F32, name="inv_sum")
+            nc.gpsimd.tensor_tensor(out=inv_sum_of[n][:], in0=row_sum_of[n][:], in1=minus_one[:], op=ALU.pow)
+
+        def turn(n, c):
+            if not 0 <= n < N_TILES:
+                return
+            if c % 2 == 0:
+                turned_of[n, c // 2] = turn_psum.tile([P, 2, PACK, P], BF16, name="turned")
+            for t in range(PACK):
+                first = T // PACK * t + P * c
+                nc.tensor.transpose(turned_of[n, c // 2][:, c % 2, t, :], e_of[n][:, first:first + P], ident[:])
+
+        def regroup(n, h, on_vector):
+            if not 0 <= n < N_TILES:
+                return
+            if h == 0:
+                grouped_of[n] = work.tile([P, N_PASS, P, PACK], BF16, name="grouped", align_bytes=64)
+            side_by_side = turned_of[n, h][:].rearrange("p c t r -> p c r t")
+            if on_vector:
+                nc.vector.tensor_copy(out=grouped_of[n][:, 2 * h:2 * h + 2], in_=side_by_side)
+            else:
+                nc.scalar.copy(out=grouped_of[n][:, 2 * h:2 * h + 2], in_=side_by_side)
+
+        def quantise(n):
+            if not 0 <= n < N_TILES:
+                return
+            codes_of[n] = work.tile([P, N_PASS, P], U32, name="e_codes", align_bytes=64)
+            scales_of[n] = work.tile([P, N_PASS, P], U8, name="e_scales", align_bytes=64)
+            nc.vector.quantize_mx(out=codes_of[n][:].rearrange("p c r -> p (c r)").bitcast(FP8X4),
+                                  scales=scales_of[n][:].rearrange("p c r -> p (c r)"),
+                                  in_=grouped_of[n][:].rearrange("p c r t -> p (c r t)"))
+
+        def multiply(n):
+            if not 0 <= n < N_TILES:
+                return
+            acc_of[n] = out_psum.tile([P, DV], F32, name="acc")
+            for c in range(N_PASS):
+                nc.tensor.matmul_mx(out=acc_of[n][:], lhsT=codes_of[n][:, c, :].bitcast(FP8X4),
+                                    lhsT_scale=scales_of[n][:, c, :],
+                                    rhs=v_codes[:, c, :].bitcast(FP8X4), rhs_scale=v_scales[:, c, :],
+                                    start=(c == 0), stop=(c == N_PASS - 1))
+
+        def finish(n):
+            if not 0 <= n < N_TILES:
+                return
+            result = work.tile([P, DV], F32)
+            nc.scalar.activation(out=result[:], in_=acc_of[n][:], func=ACT.Copy, scale=inv_sum_of[n][:, 0:1])
+            nc.sync.dma_start(out=out_tiles[n], in_=result[:])
+
+        def step(m):
+            load_mask(m + MASKS_AHEAD)
+            exponent(m - 1)
+            regroup(m - 2, 0, False)
+            regroup(m - 2, 1, False)
+            for b in range(N_BANKS):
+                mask_scores(m, b)
+                scores(m + 1, b)
+            quantise(m - 3)
+            multiply(m - 3)
+            finish(m - 3)
+            for c in range(N_PASS):
+                turn(m - 1, c)
+            row_max(m)
+
+        turn_keys(0)
+        turn_keys(1)
+        turn_queries(0)
+        step(-1)
+        for g in range(1, N_GROUPS):
+            turn_queries(g)
+        for m in range(0, 3):
+            step(m)
+        quantise_v()
+        for m in range(3, N_TILES):
+            step(m)
+
+        last = N_TILES - 1
+        exponent(last)
+        quantise(last - 2)
+        multiply(last - 2)
+        finish(last - 2)
+        regroup(last - 1, 0, True)
+        regroup(last - 1, 1, True)
+        for c in range(N_PASS):
+            turn(last, c)
+        quantise(last - 1)
+        multiply(last - 1)
+        regroup(last, 0, False)
+        regroup(last, 1, True)
+        finish(last - 1)
+        quantise(last)
+        multiply(last)
+        finish(last)

@@ -51,7 +51,7 @@ def tile_dualmodehead_kernel(tc, q, k, v, mask, mode, out):
             tc.manual_schedule():
 
         mask_of, score_of, shifted_of, row_max_of, row_sum_of = {}, {}, {}, {}, {}
-        e_of, turned_of, grouped_of, codes_of, scales_of, acc_of, inv_sum_of = {}, {}, {}, {}, {}, {}, {}
+        e_of, turned_of, grouped_of, codes_of, scales_of, acc_of, inv_sum_of, neg_max_of = {}, {}, {}, {}, {}, {}, {}, {}
 
         def load_mask(n):
             if not 0 <= n < N_TILES:
@@ -74,6 +74,8 @@ def tile_dualmodehead_kernel(tc, q, k, v, mask, mode, out):
 
         ident = keep.tile([P, P], BF16)
         make_identity(nc, ident[:])
+        ident_words = keep.tile([P, P], F32)
+        make_identity(nc, ident_words[:])
         minus_one = keep.tile([P, 1], F32)
         nc.gpsimd.memset(minus_one[:], -1.0)
 
@@ -166,16 +168,18 @@ def tile_dualmodehead_kernel(tc, q, k, v, mask, mode, out):
                 return
             row_max_of[n] = small.tile([P, 1], F32, name="row_max")
             nc.vector.tensor_reduce(out=row_max_of[n][:], in_=shifted_of[n][:], axis=mybir.AxisListType.X, op=ALU.max)
+            neg_max_of[n] = small.tile([P, 1], F32, name="neg_max")
+            nc.gpsimd.tensor_scalar(out=neg_max_of[n][:], in0=row_max_of[n][:], scalar1=-GROW, scalar2=0.0,
+                                    op0=ALU.mult, op1=ALU.add)
 
         def exponent(n):
             if not 0 <= n < N_TILES:
                 return
-            neg_max = small.tile([P, 1], F32)
-            nc.scalar.mul(out=neg_max[:], in_=row_max_of[n][:], mul=-GROW)
-            e_of[n] = work.tile([P, T], BF16, name="e_sb")
+            e_of[n] = work.tile([P, T // 2], F32, name="e_sb")
             row_sum_of[n] = small.tile([P, 1], F32, name="row_sum")
-            nc.scalar.activation(out=e_of[n][:].rearrange("p (t i) -> p t i", t=PACK),
-                                 in_=shifted_of[n][:].rearrange("p (i t) -> p t i", t=PACK), func=ACT.Exp, bias=neg_max[:, 0:1],
+            nc.scalar.activation(out=e_of[n][:].bitcast(BF16).rearrange("p (u i h) -> p u i h", u=2, h=2),
+                                 in_=shifted_of[n][:].rearrange("p (i u h) -> p u i h", u=2, h=2),
+                                 func=ACT.Exp, bias=neg_max_of[n][:, 0:1],
                                  scale=GROW, accum_out=row_sum_of[n][:])
             inv_sum_of[n] = small.tile([P, 1], F32, name="inv_sum")
             nc.gpsimd.tensor_tensor(out=inv_sum_of[n][:], in0=row_sum_of[n][:], in1=minus_one[:], op=ALU.pow)
@@ -184,17 +188,17 @@ def tile_dualmodehead_kernel(tc, q, k, v, mask, mode, out):
             if not 0 <= n < N_TILES:
                 return
             if c % 2 == 0:
-                turned_of[n, c // 2] = turn_psum.tile([P, 2, PACK, P], BF16, name="turned")
-            for t in range(PACK):
-                first = T // PACK * t + P * c
-                nc.tensor.transpose(turned_of[n, c // 2][:, c % 2, t, :], e_of[n][:, first:first + P], ident[:])
+                turned_of[n, c // 2] = turn_psum.tile([P, 2, 2, P], F32, name="turned")
+            for u in range(2):
+                first = T // 4 * u + P * c
+                nc.tensor.transpose(turned_of[n, c // 2][:, c % 2, u, :], e_of[n][:, first:first + P], ident_words[:])
 
         def regroup(n, h, on_vector):
             if not 0 <= n < N_TILES:
                 return
             if h == 0:
-                grouped_of[n] = work.tile([P, N_PASS, P, PACK], BF16, name="grouped", align_bytes=64)
-            side_by_side = turned_of[n, h][:].rearrange("p c t r -> p c r t")
+                grouped_of[n] = work.tile([P, N_PASS, P, 2], F32, name="grouped", align_bytes=64)
+            side_by_side = turned_of[n, h][:].rearrange("p c u r -> p c r u")
             if on_vector:
                 nc.vector.tensor_copy(out=grouped_of[n][:, 2 * h:2 * h + 2], in_=side_by_side)
             else:
@@ -207,7 +211,7 @@ def tile_dualmodehead_kernel(tc, q, k, v, mask, mode, out):
             scales_of[n] = work.tile([P, N_PASS, P], U8, name="e_scales", align_bytes=64)
             nc.vector.quantize_mx(out=codes_of[n][:].rearrange("p c r -> p (c r)").bitcast(FP8X4),
                                   scales=scales_of[n][:].rearrange("p c r -> p (c r)"),
-                                  in_=grouped_of[n][:].rearrange("p c r t -> p (c r t)"))
+                                  in_=grouped_of[n][:].rearrange("p c r u -> p (c r u)").bitcast(BF16))
 
         def multiply(n):
             if not 0 <= n < N_TILES:

@@ -24,6 +24,8 @@ BANK = 512
 N_BANKS = T // BANK
 GROUP = 2
 N_GROUPS = N_TILES // GROUP
+FIRST = 2 * GROUP
+REST = N_TILES - FIRST
 MASKS_AHEAD = 3
 
 SHRINK = 2.0 ** -40
@@ -35,13 +37,13 @@ FLOPS = 2 * (2 * T * T * D) + 2 * T * T * DV
 def tile_dualmodehead_kernel(tc, q, k, v, mask, mode, out):
     nc = tc.nc
     q_rows = q.flatten_outer_dims().rearrange("(p n) d -> p n d", n=N_TILES)
-    k_rows = k.flatten_outer_dims().rearrange("(j p) d -> p j d", p=P)
+    k_rows = k.flatten_outer_dims().rearrange("(b p j) d -> p b j d", p=P, j=PACK)
     v_rows = v.flatten_outer_dims().rearrange("(c p t) w -> p c t w", p=P, t=PACK)
     mask_tiles = mask.bitcast(I32).flatten_outer_dims().rearrange("(p n) (k w) -> n p k w", n=N_TILES, w=2)
     out_tiles = out.flatten_outer_dims().rearrange("(p n) w -> n p w", n=N_TILES)
 
     with tc.tile_pool(name="keep", bufs=1) as keep, \
-            tc.tile_pool(name="prep", bufs=N_GROUPS) as prep, \
+            tc.tile_pool(name="prep", bufs=3) as prep, \
             tc.tile_pool(name="mask_pool", bufs=MASKS_AHEAD + 1) as mask_pool, \
             tc.tile_pool(name="work", bufs=3) as work, \
             tc.tile_pool(name="small", bufs=6) as small, \
@@ -63,14 +65,16 @@ def tile_dualmodehead_kernel(tc, q, k, v, mask, mode, out):
 
         mode_sb = keep.tile([P, 1], BF16)
         nc.sync.dma_start(out=mode_sb[:], in_=mode.partition_broadcast(P))
-        q_ext = keep.tile([P, N_TILES, D + 1], BF16)
-        nc.sync.dma_start(out=q_ext[:, :, 0:D], in_=q_rows)
-        k_sb = keep.tile([P, N_TILES, D], BF16)
+        q_ext = keep.tile([P, FIRST, D + 1], BF16)
+        nc.sync.dma_start(out=q_ext[:, :, 0:D], in_=q_rows[:, 0:FIRST, :])
+        k_sb = keep.tile([P, N_BANKS, PACK, D], BF16)
         nc.sync.dma_start(out=k_sb[:], in_=k_rows)
         load_mask(0)
+        q_rest = keep.tile([P, REST, D], BF16)
+        nc.sync.dma_start(out=q_rest[:], in_=q_rows[:, FIRST:N_TILES, :])
+        load_mask(1)
         v_raw = keep.tile([P, N_PASS, PACK, DV], BF16)
         nc.sync.dma_start(out=v_raw[:], in_=v_rows)
-        load_mask(1)
 
         ident = keep.tile([P, P], BF16)
         make_identity(nc, ident[:])
@@ -92,26 +96,52 @@ def tile_dualmodehead_kernel(tc, q, k, v, mask, mode, out):
         nc.vector.tensor_scalar(out=w_baryon[:], in0=alpha[:], scalar1=-unit, scalar2=unit,
                                 op0=ALU.mult, op1=ALU.add)
 
-        nc.scalar.copy(out=q_ext[:, :, D:D + 1], in_=q_ext[:, :, 0:1])
         qT = keep.tile([P, N_TILES, 2, P], BF16)
         kT = keep.tile([P, T], BF16)
+        blend_of, high_of, low_of, meson_of = {}, {}, {}, {}
 
-        blend_of, high_of, low_of = {}, {}, {}
-
-        def blend_queries(g):
+        def blend_first(g):
             tiles = slice(GROUP * g, GROUP * (g + 1))
             blend_of[g] = prep.tile([P, GROUP, D], F32, name="blend")
-            nc.vector.scalar_tensor_tensor(out=blend_of[g][:], in0=q_ext[:, tiles, 1:D + 1],
-                                           scalar=w_baryon[:, 0:1], in1=meson_of[g][:],
-                                           op0=ALU.mult, op1=ALU.subtract)
             high_of[g] = prep.tile([P, GROUP, D], BF16, name="high")
-            nc.vector.scalar_tensor_tensor(out=high_of[g][:], in0=q_ext[:, tiles, 1:D + 1],
-                                           scalar=w_baryon[:, 0:1], in1=meson_of[g][:],
-                                           op0=ALU.mult, op1=ALU.subtract)
+            for result in (blend_of[g], high_of[g]):
+                nc.vector.scalar_tensor_tensor(out=result[:], in0=q_ext[:, tiles, 1:D + 1], scalar=w_baryon[:, 0:1],
+                                               in1=meson_first[:, tiles, :], op0=ALU.mult, op1=ALU.subtract)
+
+        def split_first(g):
+            low_of[g] = prep.tile([P, GROUP, D], BF16, name="low")
+            nc.vector.tensor_sub(out=low_of[g][:], in0=blend_of[g][:], in1=high_of[g][:])
+
+        def meson_part(g):
+            if not FIRST // GROUP <= g < N_GROUPS:
+                return
+            tiles = slice(GROUP * g - FIRST, GROUP * (g + 1) - FIRST)
+            meson_of[g] = prep.tile([P, GROUP, D], F32, name="meson")
+            nc.scalar.activation(out=meson_of[g][:], in_=q_rest[:, tiles, :], func=ACT.Copy, scale=w_meson[:, 0:1])
+
+        def blend_rest(g):
+            if not FIRST // GROUP <= g < N_GROUPS:
+                return
+            tiles = slice(GROUP * g - FIRST, GROUP * (g + 1) - FIRST)
+            blend_of[g] = prep.tile([P, GROUP, D], F32, name="blend")
+            nc.gpsimd.tensor_tensor(out=blend_of[g][:], in0=baryon_rest[:, tiles, :], in1=meson_of[g][:],
+                                    op=ALU.subtract)
+
+        def round_rest(g):
+            if not FIRST // GROUP <= g < N_GROUPS:
+                return
+            high_of[g] = prep.tile([P, GROUP, D], BF16, name="high")
+            nc.scalar.copy(out=high_of[g][:], in_=blend_of[g][:])
+
+        def split_rest(g):
+            if not FIRST // GROUP <= g < N_GROUPS:
+                return
             low_of[g] = prep.tile([P, GROUP, D], BF16, name="low")
             nc.gpsimd.tensor_tensor(out=low_of[g][:], in0=blend_of[g][:], in1=high_of[g][:], op=ALU.subtract)
 
         def turn_queries(g):
+            if not 0 <= g < N_GROUPS:
+                return
             tiles = slice(GROUP * g, GROUP * (g + 1))
             turned = turn_psum.tile([P, GROUP, 2, P], BF16, tag="turned")
             for i in range(GROUP):
@@ -120,24 +150,40 @@ def tile_dualmodehead_kernel(tc, q, k, v, mask, mode, out):
                 nc.tensor.transpose(turned[:, i, 1, :], low_of[g][:, i, :], ident[:])
             nc.scalar.copy(out=qT[:, tiles, :, :], in_=turned[:])
 
-        def turn_keys(h):
-            turned = turn_psum.tile([P, 8, P], BF16, tag="turned")
-            for j in range(8):
-                nc.tensor.transpose(turned[:, j, :], k_sb[:, 8 * h + j, :], ident[:])
-            nc.scalar.copy(out=kT[:, 1024 * h:1024 * (h + 1)], in_=turned[:].rearrange("p j c -> p (j c)"))
+        def turn_keys(b, on_vector):
+            turned = score_psum.tile([P, PACK, P], BF16, tag="score")
+            for j in range(PACK):
+                nc.tensor.transpose(turned[:, j, :], k_sb[:, b, j, :], ident[:])
+            columns = kT[:, BANK * b:BANK * (b + 1)].rearrange("d (p j) -> d p j", j=PACK)
+            if on_vector:
+                nc.vector.tensor_copy(out=columns, in_=turned[:].rearrange("d j p -> d p j"))
+            else:
+                nc.scalar.copy(out=columns, in_=turned[:].rearrange("d j p -> d p j"))
 
-        meson_of = {}
-        for g in range(N_GROUPS):
-            meson_of[g] = prep.tile([P, GROUP, D], F32, name="meson_part")
-            nc.scalar.activation(out=meson_of[g][:], in_=q_ext[:, GROUP * g:GROUP * (g + 1), 0:D], func=ACT.Copy,
-                                 scale=w_meson[:, 0:1])
-        for g in range(N_GROUPS):
-            blend_queries(g)
+        nc.scalar.copy(out=q_ext[:, :, D:D + 1], in_=q_ext[:, :, 0:1])
+        meson_first = keep.tile([P, FIRST, D], F32)
+        nc.scalar.activation(out=meson_first[:], in_=q_ext[:, :, 0:D], func=ACT.Copy, scale=w_meson[:, 0:1])
+        blend_first(0)
+        blend_first(1)
+        split_first(0)
+        split_first(1)
+        for b in range(N_BANKS):
+            turn_keys(b, b % 2 == 1)
+            if b == 0:
+                turn_queries(0)
+        turn_queries(1)
+
+        baryon_rest = keep.tile([P, REST, D], F32)
+        nc.gpsimd.tensor_scalar(out=baryon_rest[:, :, 0:D - 1], in0=q_rest[:, :, 1:D], scalar1=w_baryon[:, 0:1],
+                                scalar2=0.0, op0=ALU.mult, op1=ALU.add)
+        nc.gpsimd.tensor_scalar(out=baryon_rest[:, :, D - 1:D], in0=q_rest[:, :, 0:1], scalar1=w_baryon[:, 0:1],
+                                scalar2=0.0, op0=ALU.mult, op1=ALU.add)
 
         v_grouped = keep.tile([P, N_PASS, DV, PACK], BF16, align_bytes=64)
         v_codes = keep.tile([P, N_PASS, DV], U32, align_bytes=64)
         v_scales = keep.tile([P, N_PASS, DV], U8, align_bytes=64)
-        for c in range(N_PASS):
+
+        def group_v(c):
             nc.gpsimd.tensor_scalar(out=v_grouped[:, c], in0=v_raw[:, c].rearrange("p t w -> p w t"),
                                     scalar1=1.0, scalar2=0.0, op0=ALU.mult, op1=ALU.add)
 
@@ -169,8 +215,9 @@ def tile_dualmodehead_kernel(tc, q, k, v, mask, mode, out):
             row_max_of[n] = small.tile([P, 1], F32, name="row_max")
             nc.vector.tensor_reduce(out=row_max_of[n][:], in_=shifted_of[n][:], axis=mybir.AxisListType.X, op=ALU.max)
             neg_max_of[n] = small.tile([P, 1], F32, name="neg_max")
-            nc.gpsimd.tensor_scalar(out=neg_max_of[n][:], in0=row_max_of[n][:], scalar1=-GROW, scalar2=0.0,
-                                    op0=ALU.mult, op1=ALU.add)
+            engine = nc.vector if n == N_TILES - 1 else nc.gpsimd
+            engine.tensor_scalar(out=neg_max_of[n][:], in0=row_max_of[n][:], scalar1=-GROW, scalar2=0.0,
+                                 op0=ALU.mult, op1=ALU.add)
 
         def exponent(n):
             if not 0 <= n < N_TILES:
@@ -193,16 +240,13 @@ def tile_dualmodehead_kernel(tc, q, k, v, mask, mode, out):
                 first = T // 4 * u + P * c
                 nc.tensor.transpose(turned_of[n, c // 2][:, c % 2, u, :], e_of[n][:, first:first + P], ident_words[:])
 
-        def regroup(n, h, on_vector):
+        def regroup(n, h):
             if not 0 <= n < N_TILES:
                 return
             if h == 0:
                 grouped_of[n] = work.tile([P, N_PASS, P, 2], F32, name="grouped", align_bytes=64)
             side_by_side = turned_of[n, h][:].rearrange("p c u r -> p c r u")
-            if on_vector:
-                nc.vector.tensor_copy(out=grouped_of[n][:, 2 * h:2 * h + 2], in_=side_by_side)
-            else:
-                nc.scalar.copy(out=grouped_of[n][:, 2 * h:2 * h + 2], in_=side_by_side)
+            nc.scalar.copy(out=grouped_of[n][:, 2 * h:2 * h + 2], in_=side_by_side)
 
         def quantise(n):
             if not 0 <= n < N_TILES:
@@ -233,8 +277,8 @@ def tile_dualmodehead_kernel(tc, q, k, v, mask, mode, out):
         def step(m):
             load_mask(m + MASKS_AHEAD)
             exponent(m - 1)
-            regroup(m - 2, 0, False)
-            regroup(m - 2, 1, False)
+            regroup(m - 2, 0)
+            regroup(m - 2, 1)
             for b in range(N_BANKS):
                 mask_scores(m, b)
                 scores(m + 1, b)
@@ -244,33 +288,73 @@ def tile_dualmodehead_kernel(tc, q, k, v, mask, mode, out):
             for c in range(N_PASS):
                 turn(m - 1, c)
             row_max(m)
+            if m >= 0 and m % 2 == 0:
+                if m > 0:
+                    turn_queries((m - 2 + FIRST) // GROUP)
+                meson_part((m + FIRST) // GROUP)
+                blend_rest((m + FIRST) // GROUP)
+            elif m > 0:
+                round_rest((m - 1 + FIRST) // GROUP)
+                split_rest((m - 1 + FIRST) // GROUP)
+            if 0 <= m < N_PASS // 2:
+                group_v(2 * m)
+                group_v(2 * m + 1)
 
-        turn_keys(0)
-        turn_keys(1)
-        turn_queries(0)
         step(-1)
-        for g in range(1, N_GROUPS):
-            turn_queries(g)
         for m in range(0, 3):
             step(m)
         quantise_v()
-        for m in range(3, N_TILES):
+        for m in range(3, N_TILES - 1):
             step(m)
 
         last = N_TILES - 1
-        exponent(last)
+        exponent(last - 1)
+        regroup(last - 2, 0)
+        regroup(last - 2, 1)
+        for b in range(N_BANKS):
+            mask_scores(last, b)
+        quantise(last - 3)
+        multiply(last - 3)
+        finish(last - 3)
+        for c in range(N_PASS):
+            turn(last - 1, c)
+        regroup(last - 1, 0)
+        regroup(last - 1, 1)
+        row_max(last)
         quantise(last - 2)
         multiply(last - 2)
-        finish(last - 2)
-        regroup(last - 1, 0, True)
-        regroup(last - 1, 1, True)
-        for c in range(N_PASS):
-            turn(last, c)
         quantise(last - 1)
+
+        e_of[last] = work.tile([P, T // 2], F32, name="e_sb")
+        sums = small.tile([P, N_PASS], F32)
+        chunk_of, grouped_c, codes_c, scales_c = {}, {}, {}, {}
+        for c in range(N_PASS):
+            nc.scalar.activation(
+                out=e_of[last][:].bitcast(BF16).rearrange("p (u c i h) -> p u c i h", u=2, c=N_PASS, h=2)[:, :, c],
+                in_=shifted_of[last][:, K_PASS * c:K_PASS * (c + 1)].rearrange("p (i u h) -> p u i h", u=2, h=2),
+                func=ACT.Exp, bias=neg_max_of[last][:, 0:1], scale=GROW, accum_out=sums[:, c:c + 1])
+            chunk_of[c] = score_psum.tile([P, 2, P], F32, tag="score", name="chunk")
+            for u in range(2):
+                first = T // 4 * u + P * c
+                nc.tensor.transpose(chunk_of[c][:, u, :], e_of[last][:, first:first + P], ident_words[:])
+        finish(last - 2)
         multiply(last - 1)
-        regroup(last, 0, False)
-        regroup(last, 1, True)
         finish(last - 1)
-        quantise(last)
-        multiply(last)
-        finish(last)
+        acc = score_psum.tile([P, DV], F32, tag="score")
+        for c in range(N_PASS):
+            grouped_c[c] = work.tile([P, P, 2], F32, name="grouped_c", align_bytes=64)
+            nc.vector.tensor_copy(out=grouped_c[c][:], in_=chunk_of[c][:].rearrange("p u r -> p r u"))
+            codes_c[c] = work.tile([P, P], U32, name="codes_c", align_bytes=64)
+            scales_c[c] = work.tile([P, P], U8, name="scales_c", align_bytes=64)
+            nc.vector.quantize_mx(out=codes_c[c][:].bitcast(FP8X4), scales=scales_c[c][:],
+                                  in_=grouped_c[c][:].rearrange("p r u -> p (r u)").bitcast(BF16))
+            nc.tensor.matmul_mx(out=acc[:], lhsT=codes_c[c][:].bitcast(FP8X4), lhsT_scale=scales_c[c][:],
+                                rhs=v_codes[:, c, :].bitcast(FP8X4), rhs_scale=v_scales[:, c, :],
+                                start=(c == 0), stop=(c == N_PASS - 1))
+        total = small.tile([P, 1], F32)
+        nc.vector.reduce_sum(out=total[:], in_=sums[:], axis=mybir.AxisListType.X)
+        inv_total = small.tile([P, 1], F32)
+        nc.vector.reciprocal(out=inv_total[:], in_=total[:])
+        result = work.tile([P, DV], F32, name="last_result")
+        nc.vector.tensor_scalar(out=result[:], in0=acc[:], scalar1=inv_total[:, 0:1], scalar2=None, op0=ALU.mult)
+        nc.sync.dma_start(out=out_tiles[last], in_=result[:])

@@ -27,6 +27,8 @@ N_GROUPS = N_TILES // GROUP
 FIRST = 2 * GROUP
 REST = N_TILES - FIRST
 MASKS_AHEAD = 3
+SHARE_FROM = 4
+VECTOR_KEYS = (N_BANKS - 1) * BANK
 
 SHRINK = 2.0 ** -40
 GROW = 2.0 ** 40
@@ -48,12 +50,14 @@ def tile_dualmodehead_kernel(tc, q, k, v, mask, mode, out):
             tc.tile_pool(name="work", bufs=3) as work, \
             tc.tile_pool(name="small", bufs=6) as small, \
             tc.psum_pool(name="score_psum", bufs=N_BANKS) as score_psum, \
-            tc.psum_pool(name="turn_psum", bufs=3) as turn_psum, \
+            tc.psum_pool(name="late_psum", bufs=1) as late_psum, \
+            tc.psum_pool(name="turn_psum", bufs=2) as turn_psum, \
             tc.psum_pool(name="out_psum", bufs=1) as out_psum, \
             tc.manual_schedule():
 
         mask_of, score_of, shifted_of, row_max_of, row_sum_of = {}, {}, {}, {}, {}
         e_of, turned_of, grouped_of, codes_of, scales_of, acc_of, inv_sum_of, neg_max_of = {}, {}, {}, {}, {}, {}, {}, {}
+        bias_of, late_of, late_max_of, late_sum_of = {}, {}, {}, {}
 
         def load_mask(n):
             if not 0 <= n < N_TILES:
@@ -70,9 +74,9 @@ def tile_dualmodehead_kernel(tc, q, k, v, mask, mode, out):
         k_sb = keep.tile([P, N_BANKS, PACK, D], BF16)
         nc.sync.dma_start(out=k_sb[:], in_=k_rows)
         load_mask(0)
+        load_mask(1)
         q_rest = keep.tile([P, REST, D], BF16)
         nc.sync.dma_start(out=q_rest[:], in_=q_rows[:, FIRST:N_TILES, :])
-        load_mask(1)
         v_raw = keep.tile([P, N_PASS, PACK, DV], BF16)
         nc.sync.dma_start(out=v_raw[:], in_=v_rows)
 
@@ -98,7 +102,7 @@ def tile_dualmodehead_kernel(tc, q, k, v, mask, mode, out):
 
         qT = keep.tile([P, N_TILES, 2, P], BF16)
         kT = keep.tile([P, T], BF16)
-        blend_of, high_of, low_of, meson_of = {}, {}, {}, {}
+        blend_of, high_of, low_of = {}, {}, {}
 
         def blend_first(g):
             tiles = slice(GROUP * g, GROUP * (g + 1))
@@ -112,30 +116,16 @@ def tile_dualmodehead_kernel(tc, q, k, v, mask, mode, out):
             low_of[g] = prep.tile([P, GROUP, D], BF16, name="low")
             nc.vector.tensor_sub(out=low_of[g][:], in0=blend_of[g][:], in1=high_of[g][:])
 
-        def meson_part(g):
-            if not FIRST // GROUP <= g < N_GROUPS:
-                return
-            tiles = slice(GROUP * g - FIRST, GROUP * (g + 1) - FIRST)
-            meson_of[g] = prep.tile([P, GROUP, D], F32, name="meson")
-            nc.scalar.activation(out=meson_of[g][:], in_=q_rest[:, tiles, :], func=ACT.Copy, scale=w_meson[:, 0:1])
-
-        def blend_rest(g):
+        def prepare_rest(g):
             if not FIRST // GROUP <= g < N_GROUPS:
                 return
             tiles = slice(GROUP * g - FIRST, GROUP * (g + 1) - FIRST)
             blend_of[g] = prep.tile([P, GROUP, D], F32, name="blend")
-            nc.gpsimd.tensor_tensor(out=blend_of[g][:], in0=baryon_rest[:, tiles, :], in1=meson_of[g][:],
+            nc.gpsimd.tensor_tensor(out=blend_of[g][:], in0=baryon_rest[:, tiles, :], in1=meson_rest[:, tiles, :],
                                     op=ALU.subtract)
-
-        def round_rest(g):
-            if not FIRST // GROUP <= g < N_GROUPS:
-                return
             high_of[g] = prep.tile([P, GROUP, D], BF16, name="high")
-            nc.scalar.copy(out=high_of[g][:], in_=blend_of[g][:])
-
-        def split_rest(g):
-            if not FIRST // GROUP <= g < N_GROUPS:
-                return
+            nc.gpsimd.tensor_scalar(out=high_of[g][:], in0=blend_of[g][:], scalar1=1.0, scalar2=0.0,
+                                    op0=ALU.mult, op1=ALU.add)
             low_of[g] = prep.tile([P, GROUP, D], BF16, name="low")
             nc.gpsimd.tensor_tensor(out=low_of[g][:], in0=blend_of[g][:], in1=high_of[g][:], op=ALU.subtract)
 
@@ -174,26 +164,38 @@ def tile_dualmodehead_kernel(tc, q, k, v, mask, mode, out):
         turn_queries(1)
 
         baryon_rest = keep.tile([P, REST, D], F32)
-        nc.gpsimd.tensor_scalar(out=baryon_rest[:, :, 0:D - 1], in0=q_rest[:, :, 1:D], scalar1=w_baryon[:, 0:1],
-                                scalar2=0.0, op0=ALU.mult, op1=ALU.add)
-        nc.gpsimd.tensor_scalar(out=baryon_rest[:, :, D - 1:D], in0=q_rest[:, :, 0:1], scalar1=w_baryon[:, 0:1],
-                                scalar2=0.0, op0=ALU.mult, op1=ALU.add)
+        meson_rest = keep.tile([P, REST, D], F32)
+
+        def weigh_rest():
+            for result, source, factor in ((baryon_rest[:, :, 0:D - 1], q_rest[:, :, 1:D], w_baryon),
+                                           (baryon_rest[:, :, D - 1:D], q_rest[:, :, 0:1], w_baryon),
+                                           (meson_rest[:], q_rest[:], w_meson)):
+                nc.gpsimd.tensor_scalar(out=result, in0=source, scalar1=factor[:, 0:1], scalar2=0.0,
+                                        op0=ALU.mult, op1=ALU.add)
 
         v_grouped = keep.tile([P, N_PASS, DV, PACK], BF16, align_bytes=64)
         v_codes = keep.tile([P, N_PASS, DV], U32, align_bytes=64)
         v_scales = keep.tile([P, N_PASS, DV], U8, align_bytes=64)
 
         def group_v(c):
-            nc.gpsimd.tensor_scalar(out=v_grouped[:, c], in0=v_raw[:, c].rearrange("p t w -> p w t"),
-                                    scalar1=1.0, scalar2=0.0, op0=ALU.mult, op1=ALU.add)
+            side_by_side = v_raw[:, c].rearrange("p t w -> p w t")
+            if c < N_PASS // 2:
+                nc.scalar.copy(out=v_grouped[:, c], in_=side_by_side)
+            else:
+                nc.gpsimd.tensor_scalar(out=v_grouped[:, c], in0=side_by_side, scalar1=1.0, scalar2=0.0,
+                                        op0=ALU.mult, op1=ALU.add)
 
-        def quantise_v():
-            nc.vector.quantize_mx(out=v_codes[:].rearrange("p c w -> p (c w)").bitcast(FP8X4),
-                                  scales=v_scales[:].rearrange("p c w -> p (c w)"),
-                                  in_=v_grouped[:].rearrange("p c w t -> p (c w t)"))
+        def quantise_v(h):
+            passes = slice(N_PASS // 2 * h, N_PASS // 2 * (h + 1))
+            nc.vector.quantize_mx(out=v_codes[:, passes].rearrange("p c w -> p (c w)").bitcast(FP8X4),
+                                  scales=v_scales[:, passes].rearrange("p c w -> p (c w)"),
+                                  in_=v_grouped[:, passes].rearrange("p c w t -> p (c w t)"))
+
+        def shared(n):
+            return SHARE_FROM <= n < N_TILES
 
         def scores(n, b):
-            if not 0 <= n < N_TILES:
+            if not 0 <= n < N_TILES or (shared(n) and b == N_BANKS - 1):
                 return
             cols = slice(BANK * b, BANK * (b + 1))
             score_of[n, b] = score_psum.tile([P, BANK], F32, name="score")
@@ -201,7 +203,7 @@ def tile_dualmodehead_kernel(tc, q, k, v, mask, mode, out):
             nc.tensor.matmul(score_of[n, b][:], lhsT=qT[:, n, 1, :], rhs=kT[:, cols], start=False, stop=True)
 
         def mask_scores(n, b):
-            if not 0 <= n < N_TILES:
+            if not 0 <= n < N_TILES or (shared(n) and b == N_BANKS - 1):
                 return
             cols = slice(BANK * b, BANK * (b + 1))
             if b == 0:
@@ -209,27 +211,68 @@ def tile_dualmodehead_kernel(tc, q, k, v, mask, mode, out):
             nc.vector.scalar_tensor_tensor(out=shifted_of[n][:, cols], in0=mask_of[n][:, cols, 0], scalar=1.0,
                                            in1=score_of[n, b][:], op0=ALU.subtract, op1=ALU.add)
 
+        def late_bias(n):
+            if not shared(n):
+                return
+            bias_of[n] = work.tile([P, BANK], BF16, name="bias")
+            nc.scalar.activation(out=bias_of[n][:], in_=mask_of[n][:].bitcast(U32)[:, VECTOR_KEYS:T, 0], func=ACT.Copy,
+                                 bias=-1.0)
+
+        def late_scores(n):
+            if not shared(n):
+                return
+            late_of[n] = late_psum.tile([P, BANK], F32, name="late")
+            nc.tensor.matmul(late_of[n][:], lhsT=qT[:, n, 0, :], rhs=kT[:, VECTOR_KEYS:T], start=True, stop=False)
+            nc.tensor.matmul(late_of[n][:], lhsT=qT[:, n, 1, :], rhs=kT[:, VECTOR_KEYS:T], start=False, stop=False)
+
+        def late_mask(n):
+            if not shared(n):
+                return
+            nc.tensor.matmul(late_of[n][:], lhsT=ident[:], rhs=bias_of[n][:], start=False, stop=True)
+
         def row_max(n):
             if not 0 <= n < N_TILES:
                 return
             row_max_of[n] = small.tile([P, 1], F32, name="row_max")
-            nc.vector.tensor_reduce(out=row_max_of[n][:], in_=shifted_of[n][:], axis=mybir.AxisListType.X, op=ALU.max)
+            keys = VECTOR_KEYS if shared(n) else T
+            nc.vector.tensor_reduce(out=row_max_of[n][:], in_=shifted_of[n][:, 0:keys], axis=mybir.AxisListType.X,
+                                    op=ALU.max)
             neg_max_of[n] = small.tile([P, 1], F32, name="neg_max")
+            if shared(n):
+                late_max_of[n] = small.tile([P, 1], F32, name="late_max")
+                nc.vector.tensor_reduce(out=late_max_of[n][:], in_=late_of[n][:], axis=mybir.AxisListType.X, op=ALU.max)
             engine = nc.vector if n == N_TILES - 1 else nc.gpsimd
-            engine.tensor_scalar(out=neg_max_of[n][:], in0=row_max_of[n][:], scalar1=-GROW, scalar2=0.0,
-                                 op0=ALU.mult, op1=ALU.add)
+            engine.tensor_scalar(out=neg_max_of[n][:], in0=row_max_of[n][:],
+                                 scalar1=late_max_of[n][:, 0:1] if shared(n) else row_max_of[n][:, 0:1], scalar2=-GROW,
+                                 op0=ALU.max, op1=ALU.mult)
+
+        def exp_part(n, source, first, keys, row_sum):
+            words = slice(first // PACK, (first + keys) // PACK)
+            nc.scalar.activation(out=e_of[n][:].bitcast(BF16).rearrange("p (u i h) -> p u i h", u=2, h=2)[:, :, words],
+                                 in_=source.rearrange("p (i u h) -> p u i h", u=2, h=2),
+                                 func=ACT.Exp, bias=neg_max_of[n][:, 0:1], scale=GROW, accum_out=row_sum)
+
+        def late_exponent(n):
+            if not shared(n):
+                return
+            e_of[n] = work.tile([P, T // 2], F32, name="e_sb")
+            late_sum_of[n] = small.tile([P, 1], F32, name="late_sum")
+            exp_part(n, late_of[n][:], VECTOR_KEYS, BANK, late_sum_of[n][:])
 
         def exponent(n):
             if not 0 <= n < N_TILES:
                 return
-            e_of[n] = work.tile([P, T // 2], F32, name="e_sb")
+            if not shared(n):
+                e_of[n] = work.tile([P, T // 2], F32, name="e_sb")
+            keys = VECTOR_KEYS if shared(n) else T
             row_sum_of[n] = small.tile([P, 1], F32, name="row_sum")
-            nc.scalar.activation(out=e_of[n][:].bitcast(BF16).rearrange("p (u i h) -> p u i h", u=2, h=2),
-                                 in_=shifted_of[n][:].rearrange("p (i u h) -> p u i h", u=2, h=2),
-                                 func=ACT.Exp, bias=neg_max_of[n][:, 0:1],
-                                 scale=GROW, accum_out=row_sum_of[n][:])
+            exp_part(n, shifted_of[n][:, 0:keys], 0, keys, row_sum_of[n][:])
+            whole_sum = row_sum_of[n]
+            if shared(n):
+                whole_sum = small.tile([P, 1], F32, name="whole_sum")
+                nc.gpsimd.tensor_tensor(out=whole_sum[:], in0=row_sum_of[n][:], in1=late_sum_of[n][:], op=ALU.add)
             inv_sum_of[n] = small.tile([P, 1], F32, name="inv_sum")
-            nc.gpsimd.tensor_tensor(out=inv_sum_of[n][:], in0=row_sum_of[n][:], in1=minus_one[:], op=ALU.pow)
+            nc.gpsimd.tensor_tensor(out=inv_sum_of[n][:], in0=whole_sum[:], in1=minus_one[:], op=ALU.pow)
 
         def turn(n, c):
             if not 0 <= n < N_TILES:
@@ -276,51 +319,57 @@ def tile_dualmodehead_kernel(tc, q, k, v, mask, mode, out):
 
         def step(m):
             load_mask(m + MASKS_AHEAD)
+            late_exponent(m - 1)
+            late_bias(m)
             exponent(m - 1)
             regroup(m - 2, 0)
             regroup(m - 2, 1)
             for b in range(N_BANKS):
                 mask_scores(m, b)
                 scores(m + 1, b)
+                if b == 0:
+                    late_scores(m)
+                if b == 2:
+                    late_mask(m)
+            if m in (2, 3):
+                quantise_v(m - 2)
             quantise(m - 3)
             multiply(m - 3)
             finish(m - 3)
+            if m > 0 and m % 2 == 0:
+                turn_queries((m + 2) // GROUP)
             for c in range(N_PASS):
                 turn(m - 1, c)
             row_max(m)
-            if m >= 0 and m % 2 == 0:
-                if m > 0:
-                    turn_queries((m - 2 + FIRST) // GROUP)
-                meson_part((m + FIRST) // GROUP)
-                blend_rest((m + FIRST) // GROUP)
-            elif m > 0:
-                round_rest((m - 1 + FIRST) // GROUP)
-                split_rest((m - 1 + FIRST) // GROUP)
-            if 0 <= m < N_PASS // 2:
-                group_v(2 * m)
-                group_v(2 * m + 1)
+            if m == 0:
+                weigh_rest()
+            elif m % 2 == 1:
+                prepare_rest((m + 3) // GROUP)
+            if m == 1:
+                for c in range(N_PASS):
+                    group_v(c)
 
-        step(-1)
-        for m in range(0, 3):
-            step(m)
-        quantise_v()
-        for m in range(3, N_TILES - 1):
+        for m in range(-1, N_TILES - 1):
             step(m)
 
         last = N_TILES - 1
+        late_exponent(last - 1)
+        late_bias(last)
         exponent(last - 1)
+        late_scores(last)
         regroup(last - 2, 0)
         regroup(last - 2, 1)
         for b in range(N_BANKS):
             mask_scores(last, b)
-        quantise(last - 3)
-        multiply(last - 3)
-        finish(last - 3)
+        late_mask(last)
         for c in range(N_PASS):
             turn(last - 1, c)
         regroup(last - 1, 0)
         regroup(last - 1, 1)
         row_max(last)
+        quantise(last - 3)
+        multiply(last - 3)
+        finish(last - 3)
         quantise(last - 2)
         multiply(last - 2)
         quantise(last - 1)
@@ -329,10 +378,9 @@ def tile_dualmodehead_kernel(tc, q, k, v, mask, mode, out):
         sums = small.tile([P, N_PASS], F32)
         chunk_of, grouped_c, codes_c, scales_c = {}, {}, {}, {}
         for c in range(N_PASS):
-            nc.scalar.activation(
-                out=e_of[last][:].bitcast(BF16).rearrange("p (u c i h) -> p u c i h", u=2, c=N_PASS, h=2)[:, :, c],
-                in_=shifted_of[last][:, K_PASS * c:K_PASS * (c + 1)].rearrange("p (i u h) -> p u i h", u=2, h=2),
-                func=ACT.Exp, bias=neg_max_of[last][:, 0:1], scale=GROW, accum_out=sums[:, c:c + 1])
+            keys = slice(K_PASS * c, K_PASS * (c + 1))
+            exp_part(last, late_of[last][:] if c == N_PASS - 1 else shifted_of[last][:, keys], K_PASS * c, K_PASS,
+                     sums[:, c:c + 1])
             chunk_of[c] = score_psum.tile([P, 2, P], F32, tag="score", name="chunk")
             for u in range(2):
                 first = T // 4 * u + P * c

@@ -39,7 +39,7 @@ FLOPS = 2 * (2 * T * T * D) + 2 * T * T * DV
 def tile_dualmodehead_kernel(tc, q, k, v, mask, mode, out):
     nc = tc.nc
     q_rows = q.flatten_outer_dims().rearrange("(p n) d -> p n d", n=N_TILES)
-    k_rows = k.flatten_outer_dims().rearrange("(b p j) d -> p b j d", p=P, j=PACK)
+    k_rows = k.flatten_outer_dims().rearrange("(c p j) d -> p c j d", p=P, j=PACK)
     v_rows = v.flatten_outer_dims().rearrange("(c p t) w -> p c t w", p=P, t=PACK)
     mask_tiles = mask.bitcast(I32).flatten_outer_dims().rearrange("(p n) (k w) -> n p k w", n=N_TILES, w=2)
     out_tiles = out.flatten_outer_dims().rearrange("(p n) w -> n p w", n=N_TILES)
@@ -71,7 +71,7 @@ def tile_dualmodehead_kernel(tc, q, k, v, mask, mode, out):
         nc.sync.dma_start(out=mode_sb[:], in_=mode.partition_broadcast(P))
         q_ext = keep.tile([P, FIRST, D + 1], BF16)
         nc.sync.dma_start(out=q_ext[:, :, 0:D], in_=q_rows[:, 0:FIRST, :])
-        k_sb = keep.tile([P, N_BANKS, PACK, D], BF16)
+        k_sb = keep.tile([P, N_PASS, PACK, D], BF16)
         nc.sync.dma_start(out=k_sb[:], in_=k_rows)
         load_mask(0)
         load_mask(1)
@@ -140,15 +140,16 @@ def tile_dualmodehead_kernel(tc, q, k, v, mask, mode, out):
                 nc.tensor.transpose(turned[:, i, 1, :], low_of[g][:, i, :], ident[:])
             nc.scalar.copy(out=qT[:, tiles, :, :], in_=turned[:])
 
-        def turn_keys(b, on_vector):
+        def turn_keys(c, on_vector):
             turned = score_psum.tile([P, PACK, P], BF16, tag="score")
             for j in range(PACK):
-                nc.tensor.transpose(turned[:, j, :], k_sb[:, b, j, :], ident[:])
-            columns = kT[:, BANK * b:BANK * (b + 1)].rearrange("d (p j) -> d p j", j=PACK)
+                nc.tensor.transpose(turned[:, j, :], k_sb[:, c, j, :], ident[:])
+            columns = kT[:].rearrange("d (g u c p h) -> d g u c p h", g=2, u=2, c=2, h=2)[:, c // 2, :, c % 2]
+            in_pairs = turned[:].rearrange("d (u h) p -> d u p h", u=2)
             if on_vector:
-                nc.vector.tensor_copy(out=columns, in_=turned[:].rearrange("d j p -> d p j"))
+                nc.vector.tensor_copy(out=columns, in_=in_pairs)
             else:
-                nc.scalar.copy(out=columns, in_=turned[:].rearrange("d j p -> d p j"))
+                nc.scalar.copy(out=columns, in_=in_pairs)
 
         nc.scalar.copy(out=q_ext[:, :, D:D + 1], in_=q_ext[:, :, 0:1])
         meson_first = keep.tile([P, FIRST, D], F32)
@@ -157,9 +158,9 @@ def tile_dualmodehead_kernel(tc, q, k, v, mask, mode, out):
         blend_first(1)
         split_first(0)
         split_first(1)
-        for b in range(N_BANKS):
-            turn_keys(b, b % 2 == 1)
-            if b == 0:
+        for c in range(N_PASS):
+            turn_keys(c, c % 2 == 1)
+            if c == 0:
                 turn_queries(0)
         turn_queries(1)
 
@@ -191,6 +192,13 @@ def tile_dualmodehead_kernel(tc, q, k, v, mask, mode, out):
                                   scales=v_scales[:, passes].rearrange("p c w -> p (c w)"),
                                   in_=v_grouped[:, passes].rearrange("p c w t -> p (c w t)"))
 
+        def mask_pairs(keys_and_words, b):
+            keys = slice(2 * BANK * (b // 2), 2 * BANK * (b // 2 + 1))
+            return keys_and_words[:, keys, 0].rearrange("p (i u h) -> p u i h", u=2, h=2)[:, b % 2]
+
+        def pairs(scores_or_bias):
+            return scores_or_bias.rearrange("p (i h) -> p i h", h=2)
+
         def shared(n):
             return SHARE_FROM <= n < N_TILES
 
@@ -208,15 +216,15 @@ def tile_dualmodehead_kernel(tc, q, k, v, mask, mode, out):
             cols = slice(BANK * b, BANK * (b + 1))
             if b == 0:
                 shifted_of[n] = work.tile([P, T], F32, name="shifted")
-            nc.vector.scalar_tensor_tensor(out=shifted_of[n][:, cols], in0=mask_of[n][:, cols, 0], scalar=1.0,
-                                           in1=score_of[n, b][:], op0=ALU.subtract, op1=ALU.add)
+            nc.vector.scalar_tensor_tensor(out=pairs(shifted_of[n][:, cols]), in0=mask_pairs(mask_of[n][:], b),
+                                           scalar=1.0, in1=pairs(score_of[n, b][:]), op0=ALU.subtract, op1=ALU.add)
 
         def late_bias(n):
             if not shared(n):
                 return
             bias_of[n] = work.tile([P, BANK], BF16, name="bias")
-            nc.scalar.activation(out=bias_of[n][:], in_=mask_of[n][:].bitcast(U32)[:, VECTOR_KEYS:T, 0], func=ACT.Copy,
-                                 bias=-1.0)
+            nc.scalar.activation(out=pairs(bias_of[n][:]), in_=mask_pairs(mask_of[n][:].bitcast(U32), N_BANKS - 1),
+                                 func=ACT.Copy, bias=-1.0)
 
         def late_scores(n):
             if not shared(n):
@@ -246,18 +254,19 @@ def tile_dualmodehead_kernel(tc, q, k, v, mask, mode, out):
                                  scalar1=late_max_of[n][:, 0:1] if shared(n) else row_max_of[n][:, 0:1], scalar2=-GROW,
                                  op0=ALU.max, op1=ALU.mult)
 
-        def exp_part(n, source, first, keys, row_sum):
-            words = slice(first // PACK, (first + keys) // PACK)
-            nc.scalar.activation(out=e_of[n][:].bitcast(BF16).rearrange("p (u i h) -> p u i h", u=2, h=2)[:, :, words],
-                                 in_=source.rearrange("p (i u h) -> p u i h", u=2, h=2),
-                                 func=ACT.Exp, bias=neg_max_of[n][:, 0:1], scale=GROW, accum_out=row_sum)
+        def exp_part(n, result, source, row_sum):
+            nc.scalar.activation(out=result, in_=source, func=ACT.Exp, bias=neg_max_of[n][:, 0:1], scale=GROW,
+                                 accum_out=row_sum)
+
+        def e_keys(n):
+            return e_of[n][:].bitcast(BF16)
 
         def late_exponent(n):
             if not shared(n):
                 return
             e_of[n] = work.tile([P, T // 2], F32, name="e_sb")
             late_sum_of[n] = small.tile([P, 1], F32, name="late_sum")
-            exp_part(n, late_of[n][:], VECTOR_KEYS, BANK, late_sum_of[n][:])
+            exp_part(n, e_keys(n)[:, VECTOR_KEYS:T], late_of[n][:], late_sum_of[n][:])
 
         def exponent(n):
             if not 0 <= n < N_TILES:
@@ -266,7 +275,7 @@ def tile_dualmodehead_kernel(tc, q, k, v, mask, mode, out):
                 e_of[n] = work.tile([P, T // 2], F32, name="e_sb")
             keys = VECTOR_KEYS if shared(n) else T
             row_sum_of[n] = small.tile([P, 1], F32, name="row_sum")
-            exp_part(n, shifted_of[n][:, 0:keys], 0, keys, row_sum_of[n][:])
+            exp_part(n, e_keys(n)[:, 0:keys], shifted_of[n][:, 0:keys], row_sum_of[n][:])
             whole_sum = row_sum_of[n]
             if shared(n):
                 whole_sum = small.tile([P, 1], F32, name="whole_sum")
@@ -274,14 +283,17 @@ def tile_dualmodehead_kernel(tc, q, k, v, mask, mode, out):
             inv_sum_of[n] = small.tile([P, 1], F32, name="inv_sum")
             nc.gpsimd.tensor_tensor(out=inv_sum_of[n][:], in0=whole_sum[:], in1=minus_one[:], op=ALU.pow)
 
+        def words_of(n, c, u):
+            first = BANK // 2 * (2 * (c // 2) + u) + P * (c % 2)
+            return e_of[n][:, first:first + P]
+
         def turn(n, c):
             if not 0 <= n < N_TILES:
                 return
             if c % 2 == 0:
                 turned_of[n, c // 2] = turn_psum.tile([P, 2, 2, P], F32, name="turned")
             for u in range(2):
-                first = T // 4 * u + P * c
-                nc.tensor.transpose(turned_of[n, c // 2][:, c % 2, u, :], e_of[n][:, first:first + P], ident_words[:])
+                nc.tensor.transpose(turned_of[n, c // 2][:, c % 2, u, :], words_of(n, c, u), ident_words[:])
 
         def regroup(n, h):
             if not 0 <= n < N_TILES:
@@ -377,32 +389,50 @@ def tile_dualmodehead_kernel(tc, q, k, v, mask, mode, out):
         e_of[last] = work.tile([P, T // 2], F32, name="e_sb")
         sums = small.tile([P, N_PASS], F32)
         chunk_of, grouped_c, codes_c, scales_c = {}, {}, {}, {}
-        for c in range(N_PASS):
-            keys = slice(K_PASS * c, K_PASS * (c + 1))
-            exp_part(last, late_of[last][:] if c == N_PASS - 1 else shifted_of[last][:, keys], K_PASS * c, K_PASS,
-                     sums[:, c:c + 1])
+
+        def turn_chunk(c):
             chunk_of[c] = score_psum.tile([P, 2, P], F32, tag="score", name="chunk")
             for u in range(2):
-                first = T // 4 * u + P * c
-                nc.tensor.transpose(chunk_of[c][:, u, :], e_of[last][:, first:first + P], ident_words[:])
-        finish(last - 2)
-        multiply(last - 1)
-        finish(last - 1)
-        acc = score_psum.tile([P, DV], F32, tag="score")
-        for c in range(N_PASS):
+                nc.tensor.transpose(chunk_of[c][:, u, :], words_of(last, c, u), ident_words[:])
+
+        def regroup_chunk(c):
             grouped_c[c] = work.tile([P, P, 2], F32, name="grouped_c", align_bytes=64)
             nc.vector.tensor_copy(out=grouped_c[c][:], in_=chunk_of[c][:].rearrange("p u r -> p r u"))
+
+        def multiply_chunk(c, first_one, last_one):
             codes_c[c] = work.tile([P, P], U32, name="codes_c", align_bytes=64)
             scales_c[c] = work.tile([P, P], U8, name="scales_c", align_bytes=64)
             nc.vector.quantize_mx(out=codes_c[c][:].bitcast(FP8X4), scales=scales_c[c][:],
                                   in_=grouped_c[c][:].rearrange("p r u -> p (r u)").bitcast(BF16))
             nc.tensor.matmul_mx(out=acc[:], lhsT=codes_c[c][:].bitcast(FP8X4), lhsT_scale=scales_c[c][:],
                                 rhs=v_codes[:, c, :].bitcast(FP8X4), rhs_scale=v_scales[:, c, :],
-                                start=(c == 0), stop=(c == N_PASS - 1))
+                                start=first_one, stop=last_one)
+
+        late_columns, third_columns = slice(VECTOR_KEYS, T), slice(VECTOR_KEYS - BANK, VECTOR_KEYS)
+        exp_part(last, e_keys(last)[:, late_columns], late_of[last][:], sums[:, 3:4])
+        exp_part(last, e_keys(last)[:, third_columns], shifted_of[last][:, third_columns], sums[:, 2:3])
+        turn_chunk(2)
+        turn_chunk(3)
+        for c in range(2):
+            exp_part(last, e_keys(last).rearrange("p (b c k) -> p b c k", b=N_BANKS, c=2)[:, 0:2, c],
+                     shifted_of[last][:].rearrange("p (b c k) -> p b c k", b=N_BANKS, c=2)[:, 0:2, c], sums[:, c:c + 1])
+            turn_chunk(c)
+        finish(last - 2)
+        multiply(last - 1)
+        finish(last - 1)
+        acc = late_psum.tile([P, DV], F32, tag="late")
+        regroup_chunk(2)
+        regroup_chunk(3)
+        multiply_chunk(2, True, False)
+        regroup_chunk(0)
+        multiply_chunk(3, False, False)
+        multiply_chunk(0, False, False)
         total = small.tile([P, 1], F32)
         nc.vector.reduce_sum(out=total[:], in_=sums[:], axis=mybir.AxisListType.X)
+        regroup_chunk(1)
         inv_total = small.tile([P, 1], F32)
         nc.vector.reciprocal(out=inv_total[:], in_=total[:])
+        multiply_chunk(1, False, True)
         result = work.tile([P, DV], F32, name="last_result")
         nc.vector.tensor_scalar(out=result[:], in0=acc[:], scalar1=inv_total[:, 0:1], scalar2=None, op0=ALU.mult)
         nc.sync.dma_start(out=out_tiles[last], in_=result[:])

@@ -295,13 +295,16 @@ def tile_dualmodehead_kernel(tc, q, k, v, mask, mode, out):
             for u in range(2):
                 nc.tensor.transpose(turned_of[n, c // 2][:, c % 2, u, :], words_of(n, c, u), ident_words[:])
 
-        def regroup(n, h):
+        def regroup(n, h, on_vector=False):
             if not 0 <= n < N_TILES:
                 return
             if h == 0:
                 grouped_of[n] = work.tile([P, N_PASS, P, 2], F32, name="grouped", align_bytes=64)
             side_by_side = turned_of[n, h][:].rearrange("p c u r -> p c r u")
-            nc.scalar.copy(out=grouped_of[n][:, 2 * h:2 * h + 2], in_=side_by_side)
+            if on_vector:
+                nc.vector.tensor_copy(out=grouped_of[n][:, 2 * h:2 * h + 2], in_=side_by_side)
+            else:
+                nc.scalar.copy(out=grouped_of[n][:, 2 * h:2 * h + 2], in_=side_by_side)
 
         def quantise(n):
             if not 0 <= n < N_TILES:
@@ -336,18 +339,21 @@ def tile_dualmodehead_kernel(tc, q, k, v, mask, mode, out):
             exponent(m - 1)
             regroup(m - 2, 0)
             regroup(m - 2, 1)
-            for b in range(N_BANKS):
-                mask_scores(m, b)
-                scores(m + 1, b)
-                if b == 0:
-                    late_scores(m)
-                if b == 2:
-                    late_mask(m)
+            mask_scores(m, 0)
+            mask_scores(m, 1)
+            mask_scores(m, 2)
+            mask_scores(m, 3)
             if m in (2, 3):
                 quantise_v(m - 2)
             quantise(m - 3)
+            scores(m + 1, 0)
+            late_scores(m)
+            late_mask(m)
+            scores(m + 1, 1)
             multiply(m - 3)
             finish(m - 3)
+            scores(m + 1, 2)
+            scores(m + 1, 3)
             if m > 0 and m % 2 == 0:
                 turn_queries((m + 2) // GROUP)
             for c in range(N_PASS):
@@ -376,15 +382,11 @@ def tile_dualmodehead_kernel(tc, q, k, v, mask, mode, out):
         late_mask(last)
         for c in range(N_PASS):
             turn(last - 1, c)
-        regroup(last - 1, 0)
-        regroup(last - 1, 1)
         row_max(last)
         quantise(last - 3)
         multiply(last - 3)
-        finish(last - 3)
-        quantise(last - 2)
-        multiply(last - 2)
-        quantise(last - 1)
+        regroup(last - 1, 0, True)
+        regroup(last - 1, 1, True)
 
         e_of[last] = work.tile([P, T // 2], F32, name="e_sb")
         sums = small.tile([P, N_PASS], F32)
@@ -395,9 +397,12 @@ def tile_dualmodehead_kernel(tc, q, k, v, mask, mode, out):
             for u in range(2):
                 nc.tensor.transpose(chunk_of[c][:, u, :], words_of(last, c, u), ident_words[:])
 
-        def regroup_chunk(c):
-            grouped_c[c] = work.tile([P, P, 2], F32, name="grouped_c", align_bytes=64)
-            nc.vector.tensor_copy(out=grouped_c[c][:], in_=chunk_of[c][:].rearrange("p u r -> p r u"))
+        def regroup_chunk(c, on_vector):
+            grouped_c[c] = work.tile([P, P, 2], F32, name="grouped_c", align_bytes=64, bufs=N_PASS)
+            if on_vector:
+                nc.vector.tensor_copy(out=grouped_c[c][:], in_=chunk_of[c][:].rearrange("p u r -> p r u"))
+            else:
+                nc.scalar.copy(out=grouped_c[c][:], in_=chunk_of[c][:].rearrange("p u r -> p r u"))
 
         def multiply_chunk(c, first_one, last_one):
             codes_c[c] = work.tile([P, P], U32, name="codes_c", align_bytes=64)
@@ -417,22 +422,26 @@ def tile_dualmodehead_kernel(tc, q, k, v, mask, mode, out):
             exp_part(last, e_keys(last).rearrange("p (b c k) -> p b c k", b=N_BANKS, c=2)[:, 0:2, c],
                      shifted_of[last][:].rearrange("p (b c k) -> p b c k", b=N_BANKS, c=2)[:, 0:2, c], sums[:, c:c + 1])
             turn_chunk(c)
+        acc = late_psum.tile([P, DV], F32, tag="late")
+        finish(last - 3)
+        regroup_chunk(0, False)
+        regroup_chunk(1, False)
+        quantise(last - 2)
+        regroup_chunk(2, True)
+        multiply(last - 2)
+        regroup_chunk(3, True)
+        multiply_chunk(2, True, False)
+        multiply_chunk(3, False, False)
+        quantise(last - 1)
         finish(last - 2)
         multiply(last - 1)
-        finish(last - 1)
-        acc = late_psum.tile([P, DV], F32, tag="late")
-        regroup_chunk(2)
-        regroup_chunk(3)
-        multiply_chunk(2, True, False)
-        regroup_chunk(0)
-        multiply_chunk(3, False, False)
         multiply_chunk(0, False, False)
         total = small.tile([P, 1], F32)
         nc.vector.reduce_sum(out=total[:], in_=sums[:], axis=mybir.AxisListType.X)
-        regroup_chunk(1)
+        multiply_chunk(1, False, True)
         inv_total = small.tile([P, 1], F32)
         nc.vector.reciprocal(out=inv_total[:], in_=total[:])
-        multiply_chunk(1, False, True)
+        finish(last - 1)
         result = work.tile([P, DV], F32, name="last_result")
         nc.vector.tensor_scalar(out=result[:], in0=acc[:], scalar1=inv_total[:, 0:1], scalar2=None, op0=ALU.mult)
         nc.sync.dma_start(out=out_tiles[last], in_=result[:])

@@ -84,6 +84,8 @@ def tile_dualmodehead_kernel(tc, q, k, v, mask, mode, out):
         make_identity(nc, ident[:])
         ident_words = keep.tile([P, P], F32)
         make_identity(nc, ident_words[:])
+        ident_up = keep.tile([P, P], BF16)
+        nc.gpsimd.tensor_scalar(out=ident_up[:], in0=ident[:], scalar1=2.0 ** 23, scalar2=0.0, op0=ALU.mult, op1=ALU.add)
         minus_one = keep.tile([P, 1], F32)
         nc.gpsimd.memset(minus_one[:], -1.0)
 
@@ -106,6 +108,8 @@ def tile_dualmodehead_kernel(tc, q, k, v, mask, mode, out):
 
         def blend_first(g):
             tiles = slice(GROUP * g, GROUP * (g + 1))
+            nc.scalar.activation(out=meson_first[:, tiles, :], in_=q_ext[:, tiles, 0:D], func=ACT.Copy,
+                                 scale=w_meson[:, 0:1])
             blend_of[g] = prep.tile([P, GROUP, D], F32, name="blend")
             high_of[g] = prep.tile([P, GROUP, D], BF16, name="high")
             for result in (blend_of[g], high_of[g]):
@@ -116,13 +120,17 @@ def tile_dualmodehead_kernel(tc, q, k, v, mask, mode, out):
             low_of[g] = prep.tile([P, GROUP, D], BF16, name="low")
             nc.vector.tensor_sub(out=low_of[g][:], in0=blend_of[g][:], in1=high_of[g][:])
 
-        def prepare_rest(g):
+        def blend_rest(g):
             if not FIRST // GROUP <= g < N_GROUPS:
                 return
             tiles = slice(GROUP * g - FIRST, GROUP * (g + 1) - FIRST)
             blend_of[g] = prep.tile([P, GROUP, D], F32, name="blend")
             nc.gpsimd.tensor_tensor(out=blend_of[g][:], in0=baryon_rest[:, tiles, :], in1=meson_rest[:, tiles, :],
                                     op=ALU.subtract)
+
+        def split_rest(g):
+            if not FIRST // GROUP <= g < N_GROUPS:
+                return
             high_of[g] = prep.tile([P, GROUP, D], BF16, name="high")
             nc.gpsimd.tensor_scalar(out=high_of[g][:], in0=blend_of[g][:], scalar1=1.0, scalar2=0.0,
                                     op0=ALU.mult, op1=ALU.add)
@@ -140,8 +148,10 @@ def tile_dualmodehead_kernel(tc, q, k, v, mask, mode, out):
                 nc.tensor.transpose(turned[:, i, 1, :], low_of[g][:, i, :], ident[:])
             nc.scalar.copy(out=qT[:, tiles, :, :], in_=turned[:])
 
+        meson_first = keep.tile([P, FIRST, D], F32)
+
         def turn_keys(c, on_vector):
-            turned = score_psum.tile([P, PACK, P], BF16, tag="score")
+            turned = turn_psum.tile([P, PACK, P], BF16, tag="turned")
             for j in range(PACK):
                 nc.tensor.transpose(turned[:, j, :], k_sb[:, c, j, :], ident[:])
             columns = kT[:].rearrange("d (g u c p h) -> d g u c p h", g=2, u=2, c=2, h=2)[:, c // 2, :, c % 2]
@@ -152,17 +162,8 @@ def tile_dualmodehead_kernel(tc, q, k, v, mask, mode, out):
                 nc.scalar.copy(out=columns, in_=in_pairs)
 
         nc.scalar.copy(out=q_ext[:, :, D:D + 1], in_=q_ext[:, :, 0:1])
-        meson_first = keep.tile([P, FIRST, D], F32)
-        nc.scalar.activation(out=meson_first[:], in_=q_ext[:, :, 0:D], func=ACT.Copy, scale=w_meson[:, 0:1])
         blend_first(0)
-        blend_first(1)
         split_first(0)
-        split_first(1)
-        for c in range(N_PASS):
-            turn_keys(c, c % 2 == 1)
-            if c == 0:
-                turn_queries(0)
-        turn_queries(1)
 
         baryon_rest = keep.tile([P, REST, D], F32)
         meson_rest = keep.tile([P, REST, D], F32)
@@ -223,8 +224,8 @@ def tile_dualmodehead_kernel(tc, q, k, v, mask, mode, out):
             if not shared(n):
                 return
             bias_of[n] = work.tile([P, BANK], BF16, name="bias")
-            nc.scalar.activation(out=pairs(bias_of[n][:]), in_=mask_pairs(mask_of[n][:].bitcast(U32), N_BANKS - 1),
-                                 func=ACT.Copy, bias=-1.0)
+            nc.gpsimd.tensor_scalar(out=pairs(bias_of[n][:]), in0=mask_pairs(mask_of[n][:].bitcast(F32), N_BANKS - 1),
+                                    scalar1=2.0 ** 126, scalar2=-(2.0 ** -23), op0=ALU.mult, op1=ALU.add)
 
         def late_scores(n):
             if not shared(n):
@@ -236,7 +237,7 @@ def tile_dualmodehead_kernel(tc, q, k, v, mask, mode, out):
         def late_mask(n):
             if not shared(n):
                 return
-            nc.tensor.matmul(late_of[n][:], lhsT=ident[:], rhs=bias_of[n][:], start=False, stop=True)
+            nc.tensor.matmul(late_of[n][:], lhsT=ident_up[:], rhs=bias_of[n][:], start=False, stop=True)
 
         def row_max(n):
             if not 0 <= n < N_TILES:
@@ -336,6 +337,10 @@ def tile_dualmodehead_kernel(tc, q, k, v, mask, mode, out):
             load_mask(m + MASKS_AHEAD)
             late_exponent(m - 1)
             late_bias(m)
+            if m % 2 == 1:
+                split_rest((m + 3) // GROUP)
+            elif m > 0:
+                blend_rest((m + 4) // GROUP)
             exponent(m - 1)
             regroup(m - 2, 0)
             regroup(m - 2, 1)
@@ -361,13 +366,24 @@ def tile_dualmodehead_kernel(tc, q, k, v, mask, mode, out):
             row_max(m)
             if m == 0:
                 weigh_rest()
-            elif m % 2 == 1:
-                prepare_rest((m + 3) // GROUP)
+                blend_rest(FIRST // GROUP)
             if m == 1:
                 for c in range(N_PASS):
                     group_v(c)
 
-        for m in range(-1, N_TILES - 1):
+        load_mask(MASKS_AHEAD - 1)
+        turn_keys(0, False)
+        turn_keys(1, True)
+        turn_queries(0)
+        turn_keys(2, False)
+        turn_keys(3, True)
+        for b in range(N_BANKS):
+            scores(0, b)
+        blend_first(1)
+        split_first(1)
+        turn_queries(1)
+
+        for m in range(0, N_TILES - 1):
             step(m)
 
         last = N_TILES - 1

@@ -49,6 +49,7 @@ def tile_dualmodehead_kernel(tc, q, k, v, mask, mode, out):
             tc.tile_pool(name="mask_pool", bufs=MASKS_AHEAD + 1) as mask_pool, \
             tc.tile_pool(name="work", bufs=3) as work, \
             tc.tile_pool(name="small", bufs=6) as small, \
+            tc.tile_pool(name="results", bufs=N_TILES) as results, \
             tc.psum_pool(name="score_psum", bufs=N_BANKS) as score_psum, \
             tc.psum_pool(name="late_psum", bufs=1) as late_psum, \
             tc.psum_pool(name="turn_psum", bufs=2) as turn_psum, \
@@ -57,7 +58,8 @@ def tile_dualmodehead_kernel(tc, q, k, v, mask, mode, out):
 
         mask_of, score_of, shifted_of, row_max_of, row_sum_of = {}, {}, {}, {}, {}
         e_of, turned_of, grouped_of, codes_of, scales_of, acc_of, inv_sum_of, neg_max_of = {}, {}, {}, {}, {}, {}, {}, {}
-        bias_of, late_of, late_max_of, late_sum_of = {}, {}, {}, {}
+        bias_of, late_of, late_max_of, late_sum_of, result_of = {}, {}, {}, {}, {}
+        waiting = []
 
         def load_mask(n):
             if not 0 <= n < N_TILES:
@@ -329,9 +331,14 @@ def tile_dualmodehead_kernel(tc, q, k, v, mask, mode, out):
         def finish(n):
             if not 0 <= n < N_TILES:
                 return
-            result = work.tile([P, DV], F32)
-            nc.scalar.activation(out=result[:], in_=acc_of[n][:], func=ACT.Copy, scale=inv_sum_of[n][:, 0:1])
-            nc.sync.dma_start(out=out_tiles[n], in_=result[:])
+            result_of[n] = results.tile([P, DV], F32, name="result")
+            nc.scalar.activation(out=result_of[n][:], in_=acc_of[n][:], func=ACT.Copy, scale=inv_sum_of[n][:, 0:1])
+            waiting.append(n)
+
+        def store():
+            for n in waiting:
+                nc.sync.dma_start(out=out_tiles[n], in_=result_of[n][:])
+            waiting.clear()
 
         def step(m):
             load_mask(m + MASKS_AHEAD)
@@ -357,6 +364,8 @@ def tile_dualmodehead_kernel(tc, q, k, v, mask, mode, out):
             scores(m + 1, 1)
             multiply(m - 3)
             finish(m - 3)
+            if m + MASKS_AHEAD >= N_TILES - 1:
+                store()
             scores(m + 1, 2)
             scores(m + 1, 3)
             if m > 0 and m % 2 == 0:
@@ -440,6 +449,7 @@ def tile_dualmodehead_kernel(tc, q, k, v, mask, mode, out):
             turn_chunk(c)
         acc = late_psum.tile([P, DV], F32, tag="late")
         finish(last - 3)
+        store()
         regroup_chunk(0, False)
         regroup_chunk(1, False)
         quantise(last - 2)
@@ -450,6 +460,7 @@ def tile_dualmodehead_kernel(tc, q, k, v, mask, mode, out):
         multiply_chunk(3, False, False)
         quantise(last - 1)
         finish(last - 2)
+        store()
         multiply(last - 1)
         multiply_chunk(0, False, False)
         total = small.tile([P, 1], F32)
@@ -458,6 +469,7 @@ def tile_dualmodehead_kernel(tc, q, k, v, mask, mode, out):
         inv_total = small.tile([P, 1], F32)
         nc.vector.reciprocal(out=inv_total[:], in_=total[:])
         finish(last - 1)
+        store()
         result = work.tile([P, DV], F32, name="last_result")
         nc.vector.tensor_scalar(out=result[:], in0=acc[:], scalar1=inv_total[:, 0:1], scalar2=None, op0=ALU.mult)
         nc.sync.dma_start(out=out_tiles[last], in_=result[:])

@@ -70,7 +70,7 @@ def tile_dualmodehead_kernel(tc, q, k, v, mask, mode, out):
                 nc.sync.dma_start(out=mask_of[n][:, keys, :], in_=mask_tiles[n][:, keys, :])
 
         mode_sb = keep.tile([P, 1], BF16)
-        nc.sync.dma_start(out=mode_sb[:], in_=mode.partition_broadcast(P))
+        nc.scalar.dma_start(out=mode_sb[:], in_=mode.partition_broadcast(P))
         q_ext = keep.tile([P, FIRST, D + 1], BF16)
         nc.sync.dma_start(out=q_ext[:, :, 0:D], in_=q_rows[:, 0:FIRST, :])
         k_sb = keep.tile([P, N_PASS, PACK, D], BF16)
@@ -321,7 +321,10 @@ def tile_dualmodehead_kernel(tc, q, k, v, mask, mode, out):
         def multiply(n):
             if not 0 <= n < N_TILES:
                 return
-            acc_of[n] = out_psum.tile([P, DV], F32, name="acc")
+            if n == N_TILES - 2:
+                acc_of[n] = score_psum.tile([P, DV], F32, tag="score", name="spare_acc")
+            else:
+                acc_of[n] = out_psum.tile([P, DV], F32, name="acc")
             for c in range(N_PASS):
                 nc.tensor.matmul_mx(out=acc_of[n][:], lhsT=codes_of[n][:, c, :].bitcast(FP8X4),
                                     lhsT_scale=scales_of[n][:, c, :],
@@ -410,7 +413,7 @@ def tile_dualmodehead_kernel(tc, q, k, v, mask, mode, out):
         row_max(last)
         quantise(last - 3)
         multiply(last - 3)
-        regroup(last - 1, 0, True)
+        regroup(last - 1, 0)
         regroup(last - 1, 1, True)
 
         e_of[last] = work.tile([P, T // 2], F32, name="e_sb")
@@ -452,16 +455,16 @@ def tile_dualmodehead_kernel(tc, q, k, v, mask, mode, out):
         store()
         regroup_chunk(0, False)
         regroup_chunk(1, False)
+        quantise(last - 1)
         quantise(last - 2)
         regroup_chunk(2, True)
         multiply(last - 2)
         regroup_chunk(3, True)
         multiply_chunk(2, True, False)
+        multiply(last - 1)
         multiply_chunk(3, False, False)
-        quantise(last - 1)
         finish(last - 2)
         store()
-        multiply(last - 1)
         multiply_chunk(0, False, False)
         total = small.tile([P, 1], F32)
         nc.vector.reduce_sum(out=total[:], in_=sums[:], axis=mybir.AxisListType.X)

import math

import concourse.mybir as mybir
from concourse.masks import make_identity

F32 = mybir.dt.float32
BF16 = mybir.dt.bfloat16
I32 = mybir.dt.int32
U32 = mybir.dt.uint32
U8 = mybir.dt.uint8
FP8X4 = mybir.dt.float8_e4m3fn_x4
ALU = mybir.AluOpType
ACT = mybir.ActivationFunctionType

P = 128
T = 2048
D = 128
DV = 256
PACK = 4
K_PASS = P * PACK
N_PASS = T // K_PASS
N_TILES = T // P
BANK = 512
N_BANKS = T // BANK
GROUP = 2
N_GROUPS = N_TILES // GROUP
FIRST = 2 * GROUP
REST = N_TILES - FIRST
MASKS_AHEAD = 3
SHARE_FROM = 4
VECTOR_KEYS = (N_BANKS - 1) * BANK

SHRINK = 2.0 ** -40
GROW = 2.0 ** 40

FLOPS = 2 * (2 * T * T * D) + 2 * T * T * DV


def tile_dualmodehead_kernel(tc, q, k, v, mask, mode, out):
    nc = tc.nc
    q_rows = q.flatten_outer_dims().rearrange("(p n) d -> p n d", n=N_TILES)
    k_rows = k.flatten_outer_dims().rearrange("(c p j) d -> p c j d", p=P, j=PACK)
    v_rows = v.flatten_outer_dims().rearrange("(c p t) w -> p c t w", p=P, t=PACK)
    mask_tiles = mask.bitcast(I32).flatten_outer_dims().rearrange("(p n) (k w) -> n p k w", n=N_TILES, w=2)
    out_tiles = out.flatten_outer_dims().rearrange("(p n) w -> n p w", n=N_TILES)

    with tc.tile_pool(name="keep", bufs=1) as keep, \
            tc.tile_pool(name="prep", bufs=3) as prep, \
            tc.tile_pool(name="mask_pool", bufs=MASKS_AHEAD + 1) as mask_pool, \
            tc.tile_pool(name="work", bufs=3) as work, \
            tc.tile_pool(name="small", bufs=6) as small, \
            tc.tile_pool(name="results", bufs=N_TILES) as results, \
            tc.psum_pool(name="score_psum", bufs=N_BANKS) as score_psum, \
            tc.psum_pool(name="late_psum", bufs=1) as late_psum, \
            tc.psum_pool(name="turn_psum", bufs=2) as turn_psum, \
            tc.psum_pool(name="out_psum", bufs=1) as out_psum, \
            tc.manual_schedule():

        mask_of, score_of, shifted_of, row_max_of, row_sum_of = {}, {}, {}, {}, {}
        e_of, turned_of, grouped_of, codes_of, scales_of, acc_of, inv_sum_of, neg_max_of = {}, {}, {}, {}, {}, {}, {}, {}
        bias_of, late_of, late_max_of, late_sum_of, result_of = {}, {}, {}, {}, {}
        waiting = []

        def load_mask(n):
            if not 0 <= n < N_TILES:
                return
            mask_of[n] = mask_pool.tile([P, T, 2], I32, name="mask_sb")
            for h in range(2):
                keys = slice(T // 2 * h, T // 2 * (h + 1))
                nc.sync.dma_start(out=mask_of[n][:, keys, :], in_=mask_tiles[n][:, keys, :])

        mode_sb = keep.tile([P, 1], BF16)
        nc.scalar.dma_start(out=mode_sb[:], in_=mode.partition_broadcast(P))
        q_ext = keep.tile([P, FIRST, D + 1], BF16)
        nc.sync.dma_start(out=q_ext[:, :, 0:D], in_=q_rows[:, 0:FIRST, :])
        k_sb = keep.tile([P, N_PASS, PACK, D], BF16)
        nc.sync.dma_start(out=k_sb[:], in_=k_rows)
        load_mask(0)
        load_mask(1)
        q_rest = keep.tile([P, REST, D], BF16)
        nc.sync.dma_start(out=q_rest[:], in_=q_rows[:, FIRST:N_TILES, :])
        v_raw = keep.tile([P, N_PASS, PACK, DV], BF16)
        nc.sync.dma_start(out=v_raw[:], in_=v_rows)

        ident = keep.tile([P, P], BF16)
        make_identity(nc, ident[:])
        ident_words = keep.tile([P, P], F32)
        make_identity(nc, ident_words[:])
        ident_up = keep.tile([P, P], BF16)
        nc.gpsimd.tensor_scalar(out=ident_up[:], in0=ident[:], scalar1=2.0 ** 23, scalar2=0.0, op0=ALU.mult, op1=ALU.add)
        minus_one = keep.tile([P, 1], F32)
        nc.gpsimd.memset(minus_one[:], -1.0)

        exp_neg = keep.tile([P, 1], F32)
        nc.scalar.activation(out=exp_neg[:], in_=mode_sb[:], func=ACT.Exp, scale=-1.0)
        denom = keep.tile([P, 1], F32)
        nc.vector.tensor_scalar_add(out=denom[:], in0=exp_neg[:], scalar1=1.0)
        alpha = keep.tile([P, 1], F32)
        nc.vector.reciprocal(out=alpha[:], in_=denom[:])
        unit = SHRINK / math.sqrt(D)
        w_meson = keep.tile([P, 1], F32)
        nc.vector.tensor_scalar_mul(out=w_meson[:], in0=alpha[:], scalar1=unit)
        w_baryon = keep.tile([P, 1], F32)
        nc.vector.tensor_scalar(out=w_baryon[:], in0=alpha[:], scalar1=-unit, scalar2=unit,
                                op0=ALU.mult, op1=ALU.add)

        qT = keep.tile([P, N_TILES, 2, P], BF16)
        kT = keep.tile([P, T], BF16)
        blend_of, high_of, low_of = {}, {}, {}

        def blend_first(g):
            tiles = slice(GROUP * g, GROUP * (g + 1))
            nc.scalar.activation(out=meson_first[:, tiles, :], in_=q_ext[:, tiles, 0:D], func=ACT.Copy,
                                 scale=w_meson[:, 0:1])
            blend_of[g] = prep.tile([P, GROUP, D], F32, name="blend")
            high_of[g] = prep.tile([P, GROUP, D], BF16, name="high")
            for result in (blend_of[g], high_of[g]):
                nc.vector.scalar_tensor_tensor(out=result[:], in0=q_ext[:, tiles, 1:D + 1], scalar=w_baryon[:, 0:1],
                                               in1=meson_first[:, tiles, :], op0=ALU.mult, op1=ALU.subtract)

        def split_first(g):
            low_of[g] = prep.tile([P, GROUP, D], BF16, name="low")
            nc.vector.tensor_sub(out=low_of[g][:], in0=blend_of[g][:], in1=high_of[g][:])

        def blend_rest(g):
            if not FIRST // GROUP <= g < N_GROUPS:
                return
            tiles = slice(GROUP * g - FIRST, GROUP * (g + 1) - FIRST)
            blend_of[g] = prep.tile([P, GROUP, D], F32, name="blend")
            nc.gpsimd.tensor_tensor(out=blend_of[g][:], in0=baryon_rest[:, tiles, :], in1=meson_rest[:, tiles, :],
                                    op=ALU.subtract)

        def split_rest(g):
            if not FIRST // GROUP <= g < N_GROUPS:
                return
            high_of[g] = prep.tile([P, GROUP, D], BF16, name="high")
            nc.gpsimd.tensor_scalar(out=high_of[g][:], in0=blend_of[g][:], scalar1=1.0, scalar2=0.0,
                                    op0=ALU.mult, op1=ALU.add)
            low_of[g] = prep.tile([P, GROUP, D], BF16, name="low")
            nc.gpsimd.tensor_tensor(out=low_of[g][:], in0=blend_of[g][:], in1=high_of[g][:], op=ALU.subtract)

        def turn_queries(g):
            if not 0 <= g < N_GROUPS:
                return
            tiles = slice(GROUP * g, GROUP * (g + 1))
            turned = turn_psum.tile([P, GROUP, 2, P], BF16, tag="turned")
            for i in range(GROUP):
                nc.tensor.transpose(turned[:, i, 0, :], high_of[g][:, i, :], ident[:])
            for i in range(GROUP):
                nc.tensor.transpose(turned[:, i, 1, :], low_of[g][:, i, :], ident[:])
            nc.scalar.copy(out=qT[:, tiles, :, :], in_=turned[:])

        meson_first = keep.tile([P, FIRST, D], F32)

        def turn_keys(c, on_vector):
            turned = turn_psum.tile([P, PACK, P], BF16, tag="turned")
            for j in range(PACK):
                nc.tensor.transpose(turned[:, j, :], k_sb[:, c, j, :], ident[:])
            columns = kT[:].rearrange("d (g u c p h) -> d g u c p h", g=2, u=2, c=2, h=2)[:, c // 2, :, c % 2]
            in_pairs = turned[:].rearrange("d (u h) p -> d u p h", u=2)
            if on_vector:
                nc.vector.tensor_copy(out=columns, in_=in_pairs)
            else:
                nc.scalar.copy(out=columns, in_=in_pairs)

        nc.scalar.copy(out=q_ext[:, :, D:D + 1], in_=q_ext[:, :, 0:1])
        blend_first(0)
        split_first(0)

        baryon_rest = keep.tile([P, REST, D], F32)
        meson_rest = keep.tile([P, REST, D], F32)

        def weigh_rest():
            for result, source, factor in ((baryon_rest[:, :, 0:D - 1], q_rest[:, :, 1:D], w_baryon),
                                           (baryon_rest[:, :, D - 1:D], q_rest[:, :, 0:1], w_baryon),
                                           (meson_rest[:], q_rest[:], w_meson)):
                nc.gpsimd.tensor_scalar(out=result, in0=source, scalar1=factor[:, 0:1], scalar2=0.0,
                                        op0=ALU.mult, op1=ALU.add)

        v_grouped = keep.tile([P, N_PASS, DV, PACK], BF16, align_bytes=64)
        v_codes = keep.tile([P, N_PASS, DV], U32, align_bytes=64)
        v_scales = keep.tile([P, N_PASS, DV], U8, align_bytes=64)

        def group_v(c):
            side_by_side = v_raw[:, c].rearrange("p t w -> p w t")
            if c < N_PASS // 2:
                nc.scalar.copy(out=v_grouped[:, c], in_=side_by_side)
            else:
                nc.gpsimd.tensor_scalar(out=v_grouped[:, c], in0=side_by_side, scalar1=1.0, scalar2=0.0,
                                        op0=ALU.mult, op1=ALU.add)

        def quantise_v(h):
            passes = slice(N_PASS // 2 * h, N_PASS // 2 * (h + 1))
            nc.vector.quantize_mx(out=v_codes[:, passes].rearrange("p c w -> p (c w)").bitcast(FP8X4),
                                  scales=v_scales[:, passes].rearrange("p c w -> p (c w)"),
                                  in_=v_grouped[:, passes].rearrange("p c w t -> p (c w t)"))

        def mask_pairs(keys_and_words, b):
            keys = slice(2 * BANK * (b // 2), 2 * BANK * (b // 2 + 1))
            return keys_and_words[:, keys, 0].rearrange("p (i u h) -> p u i h", u=2, h=2)[:, b % 2]

        def pairs(scores_or_bias):
            return scores_or_bias.rearrange("p (i h) -> p i h", h=2)

        def shared(n):
            return SHARE_FROM <= n < N_TILES

        def scores(n, b):
            if not 0 <= n < N_TILES or (shared(n) and b == N_BANKS - 1):
                return
            cols = slice(BANK * b, BANK * (b + 1))
            score_of[n, b] = score_psum.tile([P, BANK], F32, name="score")
            nc.tensor.matmul(score_of[n, b][:], lhsT=qT[:, n, 0, :], rhs=kT[:, cols], start=True, stop=False)
            nc.tensor.matmul(score_of[n, b][:], lhsT=qT[:, n, 1, :], rhs=kT[:, cols], start=False, stop=True)

        def mask_scores(n, b):
            if not 0 <= n < N_TILES or (shared(n) and b == N_BANKS - 1):
                return
            cols = slice(BANK * b, BANK * (b + 1))
            if b == 0:
                shifted_of[n] = work.tile([P, T], F32, name="shifted")
            nc.vector.scalar_tensor_tensor(out=pairs(shifted_of[n][:, cols]), in0=mask_pairs(mask_of[n][:], b),
                                           scalar=1.0, in1=pairs(score_of[n, b][:]), op0=ALU.subtract, op1=ALU.add)

        def late_bias(n):
            if not shared(n):
                return
            bias_of[n] = work.tile([P, BANK], BF16, name="bias")
            nc.gpsimd.tensor_scalar(out=pairs(bias_of[n][:]), in0=mask_pairs(mask_of[n][:].bitcast(F32), N_BANKS - 1),
                                    scalar1=2.0 ** 126, scalar2=-(2.0 ** -23), op0=ALU.mult, op1=ALU.add)

        def late_scores(n):
            if not shared(n):
                return
            late_of[n] = late_psum.tile([P, BANK], F32, name="late")
            nc.tensor.matmul(late_of[n][:], lhsT=qT[:, n, 0, :], rhs=kT[:, VECTOR_KEYS:T], start=True, stop=False)
            nc.tensor.matmul(late_of[n][:], lhsT=qT[:, n, 1, :], rhs=kT[:, VECTOR_KEYS:T], start=False, stop=False)

        def late_mask(n):
            if not shared(n):
                return
            nc.tensor.matmul(late_of[n][:], lhsT=ident_up[:], rhs=bias_of[n][:], start=False, stop=True)

        def row_max(n):
            if not 0 <= n < N_TILES:
                return
            row_max_of[n] = small.tile([P, 1], F32, name="row_max")
            keys = VECTOR_KEYS if shared(n) else T
            nc.vector.tensor_reduce(out=row_max_of[n][:], in_=shifted_of[n][:, 0:keys], axis=mybir.AxisListType.X,
                                    op=ALU.max)
            neg_max_of[n] = small.tile([P, 1], F32, name="neg_max")
            if shared(n):
                late_max_of[n] = small.tile([P, 1], F32, name="late_max")
                nc.vector.tensor_reduce(out=late_max_of[n][:], in_=late_of[n][:], axis=mybir.AxisListType.X, op=ALU.max)
            engine = nc.vector if n == N_TILES - 1 else nc.gpsimd
            engine.tensor_scalar(out=neg_max_of[n][:], in0=row_max_of[n][:],
                                 scalar1=late_max_of[n][:, 0:1] if shared(n) else row_max_of[n][:, 0:1], scalar2=-GROW,
                                 op0=ALU.max, op1=ALU.mult)

        def exp_part(n, result, source, row_sum):
            nc.scalar.activation(out=result, in_=source, func=ACT.Exp, bias=neg_max_of[n][:, 0:1], scale=GROW,
                                 accum_out=row_sum)

        def e_keys(n):
            return e_of[n][:].bitcast(BF16)

        def late_exponent(n):
            if not shared(n):
                return
            e_of[n] = work.tile([P, T // 2], F32, name="e_sb")
            late_sum_of[n] = small.tile([P, 1], F32, name="late_sum")
            exp_part(n, e_keys(n)[:, VECTOR_KEYS:T], late_of[n][:], late_sum_of[n][:])

        def exponent(n):
            if not 0 <= n < N_TILES:
                return
            if not shared(n):
                e_of[n] = work.tile([P, T // 2], F32, name="e_sb")
            keys = VECTOR_KEYS if shared(n) else T
            row_sum_of[n] = small.tile([P, 1], F32, name="row_sum")
            exp_part(n, e_keys(n)[:, 0:keys], shifted_of[n][:, 0:keys], row_sum_of[n][:])
            whole_sum = row_sum_of[n]
            if shared(n):
                whole_sum = small.tile([P, 1], F32, name="whole_sum")
                nc.gpsimd.tensor_tensor(out=whole_sum[:], in0=row_sum_of[n][:], in1=late_sum_of[n][:], op=ALU.add)
            inv_sum_of[n] = small.tile([P, 1], F32, name="inv_sum")
            nc.gpsimd.tensor_tensor(out=inv_sum_of[n][:], in0=whole_sum[:], in1=minus_one[:], op=ALU.pow)

        def words_of(n, c, u):
            first = BANK // 2 * (2 * (c // 2) + u) + P * (c % 2)
            return e_of[n][:, first:first + P]

        def turn(n, c):
            if not 0 <= n < N_TILES:
                return
            if c % 2 == 0:
                turned_of[n, c // 2] = turn_psum.tile([P, 2, 2, P], F32, name="turned")
            for u in range(2):
                nc.tensor.transpose(turned_of[n, c // 2][:, c % 2, u, :], words_of(n, c, u), ident_words[:])

        def regroup(n, h, on_vector=False):
            if not 0 <= n < N_TILES:
                return
            if h == 0:
                grouped_of[n] = work.tile([P, N_PASS, P, 2], F32, name="grouped", align_bytes=64)
            side_by_side = turned_of[n, h][:].rearrange("p c u r -> p c r u")
            if on_vector:
                nc.vector.tensor_copy(out=grouped_of[n][:, 2 * h:2 * h + 2], in_=side_by_side)
            else:
                nc.scalar.copy(out=grouped_of[n][:, 2 * h:2 * h + 2], in_=side_by_side)

        def quantise(n):
            if not 0 <= n < N_TILES:
                return
            codes_of[n] = work.tile([P, N_PASS, P], U32, name="e_codes", align_bytes=64)
            scales_of[n] = work.tile([P, N_PASS, P], U8, name="e_scales", align_bytes=64)
            nc.vector.quantize_mx(out=codes_of[n][:].rearrange("p c r -> p (c r)").bitcast(FP8X4),
                                  scales=scales_of[n][:].rearrange("p c r -> p (c r)"),
                                  in_=grouped_of[n][:].rearrange("p c r u -> p (c r u)").bitcast(BF16))

        def multiply(n):
            if not 0 <= n < N_TILES:
                return
            if n == N_TILES - 2:
                acc_of[n] = score_psum.tile([P, DV], F32, tag="score", name="spare_acc")
            else:
                acc_of[n] = out_psum.tile([P, DV], F32, name="acc")
            for c in range(N_PASS):
                nc.tensor.matmul_mx(out=acc_of[n][:], lhsT=codes_of[n][:, c, :].bitcast(FP8X4),
                                    lhsT_scale=scales_of[n][:, c, :],
                                    rhs=v_codes[:, c, :].bitcast(FP8X4), rhs_scale=v_scales[:, c, :],
                                    start=(c == 0), stop=(c == N_PASS - 1))

        def finish(n):
            if not 0 <= n < N_TILES:
                return
            result_of[n] = results.tile([P, DV], F32, name="result")
            nc.scalar.activation(out=result_of[n][:], in_=acc_of[n][:], func=ACT.Copy, scale=inv_sum_of[n][:, 0:1])
            waiting.append(n)

        def store():
            for n in waiting:
                nc.sync.dma_start(out=out_tiles[n], in_=result_of[n][:])
            waiting.clear()

        def step(m):
            load_mask(m + MASKS_AHEAD)
            late_exponent(m - 1)
            late_bias(m)
            if m % 2 == 1:
                split_rest((m + 3) // GROUP)
            elif m > 0:
                blend_rest((m + 4) // GROUP)
            exponent(m - 1)
            regroup(m - 2, 0)
            regroup(m - 2, 1)
            mask_scores(m, 0)
            mask_scores(m, 1)
            mask_scores(m, 2)
            mask_scores(m, 3)
            if m in (2, 3):
                quantise_v(m - 2)
            quantise(m - 3)
            scores(m + 1, 0)
            late_scores(m)
            late_mask(m)
            scores(m + 1, 1)
            multiply(m - 3)
            finish(m - 3)
            if m + MASKS_AHEAD >= N_TILES - 1:
                store()
            scores(m + 1, 2)
            scores(m + 1, 3)
            if m > 0 and m % 2 == 0:
                turn_queries((m + 2) // GROUP)
            for c in range(N_PASS):
                turn(m - 1, c)
            row_max(m)
            if m == 0:
                weigh_rest()
                blend_rest(FIRST // GROUP)
            if m == 1:
                for c in range(N_PASS):
                    group_v(c)

        load_mask(MASKS_AHEAD - 1)
        turn_keys(0, False)
        turn_keys(1, True)
        turn_queries(0)
        turn_keys(2, False)
        turn_keys(3, True)
        for b in range(N_BANKS):
            scores(0, b)
        blend_first(1)
        split_first(1)
        turn_queries(1)

        for m in range(0, N_TILES - 1):
            step(m)

        last = N_TILES - 1
        late_exponent(last - 1)
        late_bias(last)
        exponent(last - 1)
        late_scores(last)
        regroup(last - 2, 0)
        regroup(last - 2, 1)
        for b in range(N_BANKS):
            mask_scores(last, b)
        late_mask(last)
        for c in range(N_PASS):
            turn(last - 1, c)
        row_max(last)
        quantise(last - 3)
        multiply(last - 3)
        regroup(last - 1, 0)
        regroup(last - 1, 1, True)

        e_of[last] = work.tile([P, T // 2], F32, name="e_sb")
        sums = small.tile([P, N_PASS], F32)
        chunk_of, grouped_c, codes_c, scales_c = {}, {}, {}, {}

        def turn_chunk(c):
            chunk_of[c] = score_psum.tile([P, 2, P], F32, tag="score", name="chunk")
            for u in range(2):
                nc.tensor.transpose(chunk_of[c][:, u, :], words_of(last, c, u), ident_words[:])

        def regroup_chunk(c, on_vector):
            grouped_c[c] = work.tile([P, P, 2], F32, name="grouped_c", align_bytes=64, bufs=N_PASS)
            if on_vector:
                nc.vector.tensor_copy(out=grouped_c[c][:], in_=chunk_of[c][:].rearrange("p u r -> p r u"))
            else:
                nc.scalar.copy(out=grouped_c[c][:], in_=chunk_of[c][:].rearrange("p u r -> p r u"))

        def multiply_chunk(c, first_one, last_one):
            codes_c[c] = work.tile([P, P], U32, name="codes_c", align_bytes=64)
            scales_c[c] = work.tile([P, P], U8, name="scales_c", align_bytes=64)
            nc.vector.quantize_mx(out=codes_c[c][:].bitcast(FP8X4), scales=scales_c[c][:],
                                  in_=grouped_c[c][:].rearrange("p r u -> p (r u)").bitcast(BF16))
            nc.tensor.matmul_mx(out=acc[:], lhsT=codes_c[c][:].bitcast(FP8X4), lhsT_scale=scales_c[c][:],
                                rhs=v_codes[:, c, :].bitcast(FP8X4), rhs_scale=v_scales[:, c, :],
                                start=first_one, stop=last_one)

        late_columns, third_columns = slice(VECTOR_KEYS, T), slice(VECTOR_KEYS - BANK, VECTOR_KEYS)
        exp_part(last, e_keys(last)[:, late_columns], late_of[last][:], sums[:, 3:4])
        exp_part(last, e_keys(last)[:, third_columns], shifted_of[last][:, third_columns], sums[:, 2:3])
        turn_chunk(2)
        turn_chunk(3)
        for c in range(2):
            exp_part(last, e_keys(last).rearrange("p (b c k) -> p b c k", b=N_BANKS, c=2)[:, 0:2, c],
                     shifted_of[last][:].rearrange("p (b c k) -> p b c k", b=N_BANKS, c=2)[:, 0:2, c], sums[:, c:c + 1])
            turn_chunk(c)
        acc = late_psum.tile([P, DV], F32, tag="late")
        finish(last - 3)
        store()
        regroup_chunk(0, False)
        regroup_chunk(1, False)
        quantise(last - 1)
        quantise(last - 2)
        regroup_chunk(2, True)
        multiply(last - 2)
        regroup_chunk(3, True)
        multiply_chunk(2, True, False)
        multiply(last - 1)
        multiply_chunk(3, False, False)
        finish(last - 2)
        store()
        multiply_chunk(0, False, False)
        total = small.tile([P, 1], F32)
        nc.vector.reduce_sum(out=total[:], in_=sums[:], axis=mybir.AxisListType.X)
        multiply_chunk(1, False, True)
        inv_total = small.tile([P, 1], F32)
        nc.vector.reciprocal(out=inv_total[:], in_=total[:])
        finish(last - 1)
        store()
        result = work.tile([P, DV], F32, name="last_result")
        nc.vector.tensor_scalar(out=result[:], in0=acc[:], scalar1=inv_total[:, 0:1], scalar2=None, op0=ALU.mult)
        nc.sync.dma_start(out=out_tiles[last], in_=result[:])
